import numpy as np
import ml_dtypes


def mxq(x, axis, fmt="e4m3"):
    dtype, down = {"e4m3": (ml_dtypes.float8_e4m3fn, 7), "e5m2": (ml_dtypes.float8_e5m2, 14)}[fmt]
    v = np.moveaxis(np.asarray(x, np.float32).astype(ml_dtypes.bfloat16).astype(np.float64), axis, -1)
    blocks = v.reshape(v.shape[:-1] + (-1, 32))
    amax = np.abs(blocks).max(-1, keepdims=True)
    byte = np.maximum(np.where(amax > 0, np.frexp(amax)[1] - 1 + 127, 0) - down, 1)
    scale = np.exp2(byte - 127.0)
    codes = (blocks / scale).astype(np.float32).astype(dtype).astype(np.float64)
    return np.moveaxis((codes * scale).reshape(v.shape), -1, axis)


WIDE = False


def mx_kscale(k):
    if not WIDE:
        return np.ones(k)
    levels = np.array([10, -10, 5, -5, 0])
    a = np.random.permutation(np.resize(levels, k // 512 * 4)).reshape(k // 512, 4)
    idx = np.arange(k)
    return np.exp2(a[idx // 512, idx % 128 // 32])


BF16 = ml_dtypes.bfloat16


def bf(x):
    return np.asarray(x, np.float32).astype(BF16)


def f64(x):
    return np.asarray(x).astype(np.float64)


E2M1 = np.array([0.0, 0.5, 1.0, 1.5, 2.0, 3.0, 4.0, 6.0, -0.0, -0.5, -1.0, -1.5, -2.0, -3.0, -4.0, -6.0])


def pack_weight(w, fmt):
    k, n = w.shape
    w = f64(bf(w)).reshape(k // 32, 32, n)
    amax = np.abs(w).max(1)
    if fmt == "e4m3":
        byte = np.frexp(amax)[1] - 1 + 127 - 7
    else:
        mant, ex = np.frexp(amax / 6.0)
        byte = np.where(mant > 0.5, ex, ex - 1) + 127
    byte = np.clip(np.where(amax > 0, byte, 1), 1, 254)
    scaled = (w * np.exp2(127.0 - byte)[:, None, :]).reshape(k, n).astype(np.float32)
    by_word = np.ascontiguousarray(scaled.reshape(k // 512, 128, 4, n).transpose(0, 1, 3, 2))
    if fmt == "e4m3":
        words = by_word.astype(ml_dtypes.float8_e4m3fn).view(np.uint8)
    else:
        c = by_word.astype(ml_dtypes.float4_e2m1fn).view(np.uint8) & 0xF
        words = c[..., 0::2] | (c[..., 1::2] << 4)
    return np.ascontiguousarray(words), np.ascontiguousarray(byte.astype(np.uint8).reshape(k // 512, 16, n))


def unpack_weight(words, scales, fmt):
    g, p, n, _ = words.shape
    if fmt == "e4m3":
        vals = np.ascontiguousarray(words).view(ml_dtypes.float8_e4m3fn).astype(np.float64)
    else:
        nib = np.empty((g, p, n, 4), np.uint8)
        nib[..., 0::2] = words & 0xF
        nib[..., 1::2] = words >> 4
        vals = E2M1[nib]
    vals = vals * np.repeat(np.exp2(scales.astype(np.float64) - 127.0), 8, axis=1)[..., None]
    return vals.transpose(0, 1, 3, 2).reshape(g * 512, n)

def pack4(w):
    words, scales = pack_weight(w, "e2m1")
    return words.reshape(words.shape[0], 128, -1), scales


def unpack4(words, scales):
    return unpack_weight(words.reshape(words.shape[0], 128, -1, 2), scales, "e2m1")


B, S, E, H, DH, ROT, MP = 4, 2048, 512, 4, 64, 32, 2
HD = H * DH
LOC = HD // MP


def rope_sincos():
    inv_freq = 1.0 / (10000.0 ** (np.arange(0, ROT, 2) / ROT))
    ang = np.arange(S)[:, None] * inv_freq[None, :]
    return np.sin(ang), np.cos(ang)


def apply_rope(x, sin, cos):
    sin2 = np.repeat(sin, 2, axis=-1)[None, :, None, :]
    cos2 = np.repeat(cos, 2, axis=-1)[None, :, None, :]
    x1 = x[..., ::2]
    x2 = x[..., 1::2]
    rot = np.stack((-x2, x1), axis=-1).reshape(x.shape)
    return x * cos2 + rot * sin2


def setup_inputs():
    s = mx_kscale(E)
    hidden_states = bf(np.random.standard_normal((B, S, E)) * s)
    w = np.random.standard_normal((3 * HD, E)) / np.sqrt(E) / s[None, :]
    words, scales = pack4(np.ascontiguousarray(w.T))
    return {"hidden_states": hidden_states,
            "W_qkv_words": words,
            "W_qkv_scales": scales}


def reference(hidden_states, W_qkv_words, W_qkv_scales):
    qkv = mxq(f64(hidden_states), 2, "e4m3") @ unpack4(W_qkv_words, W_qkv_scales)
    qkv = qkv.reshape(B, S, MP, 3 * LOC)
    q, k, v = np.split(qkv, 3, axis=-1)
    q = q.reshape(B, S, H, DH)
    k = k.reshape(B, S, H, DH)
    v = v.reshape(B, S, H, DH)
    sin, cos = rope_sincos()
    q = np.concatenate([apply_rope(q[..., :ROT], sin, cos), q[..., ROT:]], axis=-1)
    k = np.concatenate([apply_rope(k[..., :ROT], sin, cos), k[..., ROT:]], axis=-1)
    return q, k, v

@@ -1,0 +1,252 @@
+from contextlib import ExitStack
+
+import concourse.mybir as mybir
+from concourse.masks import make_identity
+
+F32 = mybir.dt.float32
+BF16 = mybir.dt.bfloat16
+I32 = mybir.dt.int32
+U32 = mybir.dt.uint32
+U8 = mybir.dt.uint8
+FP8X4 = mybir.dt.float8_e4m3fn_x4
+FP4X4 = mybir.dt.float4_e2m1fn_x4
+ALU = mybir.AluOpType
+ACT = mybir.ActivationFunctionType
+
+P = 128
+BATCH, SEQ, EMBED = 4, 2048, 512
+HEADS, HEAD_DIM, ROT = 4, 64, 32
+WIDTH = HEADS * HEAD_DIM
+ANGLES = ROT // 2
+SLOTS = SEQ // P
+PAIR = 2
+CHUNK = 4
+CHUNKS_PER_BATCH = SLOTS // CHUNK
+N_CHUNKS = BATCH * CHUNKS_PER_BATCH
+N_PAIRS = N_CHUNKS * CHUNK // PAIR
+TWO_PI = 6.283185307179586
+ROUND = 12582912.0
+
+FLOPS = 2 * BATCH * SEQ * EMBED * 3 * WIDTH
+
+
+def split_constant(value):
+    scale = 1.0
+    while value * scale < 2048.0:
+        scale *= 2.0
+    high = round(value * scale) / scale
+    return high, value - high
+
+
+def regroup_columns(nc, dst, src):
+    natural = src.rearrange("p (g k s f w) -> p g k s f w", g=2, k=3, s=2, f=2)
+    blocks = dst.rearrange("p (n c) -> p n c", n=6)
+    for half in range(2):
+        for kind in range(2):
+            nc.vector.tensor_copy(
+                out=blocks[:, 2 * half + kind, :].rearrange("p (g s w) -> p g s w", g=2, s=2),
+                in_=natural[:, :, kind, :, half, :],
+            )
+    nc.vector.tensor_copy(
+        out=blocks[:, 4:6, :],
+        in_=src.rearrange("p (g k c) -> p g k c", g=2, k=3)[:, :, 2, :],
+    )
+
+
+def tile_progenattention_pa_t_kernel(
+    tc, hidden_states, W_qkv_words, W_qkv_scales, out_0, out_1, out_2
+):
+    nc = tc.nc
+    x_dram = hidden_states.rearrange("b (p t) e -> b p t e", t=SLOTS)
+    out_dram = [o.rearrange("b (p t) h d -> b p t (h d)", t=SLOTS) for o in (out_0, out_1, out_2)]
+
+    with ExitStack() as ctx:
+        const = ctx.enter_context(tc.tile_pool(name="const", bufs=1))
+        x_pool = ctx.enter_context(tc.tile_pool(name="x", bufs=N_CHUNKS))
+        work = ctx.enter_context(tc.tile_pool(name="work", bufs=3))
+        out_pool = ctx.enter_context(tc.tile_pool(name="out", bufs=8))
+        psum = ctx.enter_context(tc.psum_pool(name="psum", bufs=2))
+
+        x_tiles = []
+
+        def load_chunk(chunk):
+            batch, part = divmod(chunk, CHUNKS_PER_BATCH)
+            x_sb = x_pool.tile([P, CHUNK, EMBED], BF16)
+            nc.sync.dma_start(
+                out=x_sb[:], in_=x_dram[batch, :, part * CHUNK : (part + 1) * CHUNK, :]
+            )
+            x_tiles.append(x_sb)
+
+        w_scales_in = const.tile([P, 3 * WIDTH], U8, align_bytes=64)
+        nc.vector.memset(w_scales_in[:].bitcast(I32), 0)
+        w_words_in = const.tile([P, 2 * 3 * WIDTH], U8, align_bytes=64)
+        load_chunk(0)
+        for quadrant in range(4):
+            nc.sync.dma_start(
+                out=w_scales_in[32 * quadrant : 32 * quadrant + 4, :].bitcast(I32),
+                in_=W_qkv_scales[0, 4 * quadrant : 4 * quadrant + 4, :].bitcast(I32),
+            )
+        nc.sync.dma_start(out=w_words_in[:].bitcast(I32), in_=W_qkv_words[0].bitcast(I32))
+        for chunk in range(1, N_CHUNKS):
+            load_chunk(chunk)
+
+        warm = const.tile([P, 1], F32)
+        nc.vector.memset(warm[:], 0.0)
+        nc.scalar.activation(out=warm[:], in_=warm[:], func=ACT.Sin)
+
+        position_i = const.tile([P, SLOTS], I32)
+        nc.gpsimd.iota(position_i[:], pattern=[[1, SLOTS]], base=0, channel_multiplier=SLOTS)
+        ident = const.tile([P, P], F32)
+        make_identity(nc, ident[:])
+        position = const.tile([P, SLOTS], F32)
+        nc.vector.tensor_copy(out=position[:], in_=position_i[:])
+
+        turns_high = const.tile([P, SLOTS, ANGLES], F32)
+        turns_low = const.tile([P, SLOTS, ANGLES], F32)
+        for j in range(ANGLES):
+            high, low = split_constant(1.0 / (10000.0 ** (2 * j / ROT)) / TWO_PI)
+            nc.vector.tensor_scalar_mul(out=turns_high[:, :, j], in0=position[:], scalar1=high)
+            nc.vector.tensor_scalar_mul(out=turns_low[:, :, j], in0=position[:], scalar1=low)
+
+        def drop_whole_turns(name, turns):
+            whole = const.tile([P, SLOTS, ANGLES], F32, name=name + "_whole")
+            nc.vector.tensor_scalar(
+                out=whole[:], in0=turns[:], scalar1=ROUND, scalar2=ROUND,
+                op0=ALU.add, op1=ALU.subtract,
+            )
+            rest = const.tile([P, SLOTS, ANGLES], F32, name=name)
+            nc.vector.tensor_tensor(out=rest[:], in0=turns[:], in1=whole[:], op=ALU.subtract)
+            return rest
+
+        high_rest = drop_whole_turns("high_rest", turns_high)
+        turns = const.tile([P, SLOTS, ANGLES], F32)
+        nc.vector.tensor_tensor(out=turns[:], in0=high_rest[:], in1=turns_low[:], op=ALU.add)
+        sin_turns = drop_whole_turns("sin_turns", turns)
+        quarter_on = const.tile([P, SLOTS, ANGLES], F32)
+        nc.vector.tensor_scalar_add(out=quarter_on[:], in0=sin_turns[:], scalar1=0.25)
+        cos_turns = drop_whole_turns("cos_turns", quarter_on)
+
+        sin_table = const.tile([P, SLOTS, ANGLES, 2], F32)
+        cos_table = const.tile([P, SLOTS, ROT], F32)
+        nc.scalar.activation(
+            out=sin_table[:, :, :, 0], in_=sin_turns[:], func=ACT.Sin, scale=-TWO_PI
+        )
+        nc.scalar.activation(
+            out=sin_table[:, :, :, 1], in_=sin_turns[:], func=ACT.Sin, scale=TWO_PI
+        )
+        nc.scalar.activation(
+            out=cos_table[:].rearrange("p t (j e) -> p t j e", e=2),
+            in_=cos_turns[:].unsqueeze(3).to_broadcast([P, SLOTS, ANGLES, 2]),
+            func=ACT.Sin,
+            scale=TWO_PI,
+        )
+
+        w_words = const.tile([P, 2 * 3 * WIDTH], U8, align_bytes=64)
+        w_scales = const.tile([P, 3 * WIDTH], U8, align_bytes=64)
+        regroup_columns(nc, w_words[:].bitcast(I32), w_words_in[:].bitcast(I32))
+        regroup_columns(nc, w_scales[:].bitcast(I32), w_scales_in[:].bitcast(I32))
+
+        grouped_of = {}
+        banks_of = {}
+        out_of = {}
+        cross_of = {}
+
+        def transpose_pair(pair):
+            chunk, first = divmod(pair * PAIR, CHUNK)
+            flipped = psum.tile([P, PAIR, 2, P], F32)
+            for c in range(PAIR):
+                words = x_tiles[chunk][:, first + c, :].bitcast(F32)
+                for odd in range(2):
+                    nc.tensor.transpose(flipped[:, c, odd, :], words[:, odd : EMBED // 2 : 2], ident[:])
+            grouped = work.tile([P, PAIR * P * 4], BF16, align_bytes=64)
+            nc.scalar.copy(
+                out=grouped[:].bitcast(F32).rearrange("p (c r w) -> p c r w", c=PAIR, w=2),
+                in_=flipped[:].rearrange("p c w r -> p c r w"),
+            )
+            grouped_of[pair] = grouped
+
+        def project_pair(pair):
+            codes = work.tile([P, PAIR * P], U32, align_bytes=64)
+            scales = work.tile([P, PAIR * P], U8, align_bytes=64)
+            nc.vector.quantize_mx(
+                out=codes[:].bitcast(FP8X4), scales=scales[:], in_=grouped_of[pair][:]
+            )
+            rotated = psum.tile([P, PAIR, WIDTH], F32)
+            others = psum.tile([P, PAIR, WIDTH], F32)
+            values = psum.tile([P, PAIR, WIDTH], F32)
+            banks_of[pair] = (rotated, others, values)
+            for c in range(PAIR):
+                tokens = slice(c * P, (c + 1) * P)
+                for n, bank in enumerate(banks_of[pair]):
+                    nc.tensor.matmul_mx(
+                        out=bank[:, c, :],
+                        lhsT=codes[:, tokens].bitcast(FP8X4),
+                        lhsT_scale=scales[:, tokens],
+                        rhs=w_words[:, 2 * n * WIDTH : 2 * (n + 1) * WIDTH].bitcast(FP4X4),
+                        rhs_scale=w_scales[:, n * WIDTH : (n + 1) * WIDTH],
+                        start=True,
+                        stop=True,
+                    )
+
+        def finish_pair(pair):
+            chunk, first = divmod(pair * PAIR, CHUNK)
+            if first == 0:
+                out_sb = out_pool.tile([P, 3, CHUNK, HEADS, HEAD_DIM], F32)
+                cross = work.tile([P, CHUNK, 2 * HEADS * ROT], F32)
+                out_of[chunk] = out_sb
+                cross_of[chunk] = cross
+            out_sb = out_of[chunk]
+            cross = cross_of[chunk]
+            rotated, others, values = banks_of[pair]
+            for c in range(PAIR):
+                slot = (chunk % CHUNKS_PER_BATCH) * CHUNK + first + c
+                nc.vector.tensor_tensor(
+                    out=out_sb[:, 0:2, first + c, :, 0:ROT],
+                    in0=rotated[:, c, :].rearrange("p (k h i) -> p k h i", k=2, h=HEADS),
+                    in1=cos_table[:, slot, :].unsqueeze(1).unsqueeze(1).to_broadcast([P, 2, HEADS, ROT]),
+                    op=ALU.mult,
+                )
+                nc.vector.tensor_tensor(
+                    out=cross[:, first + c, :].rearrange("p (m j e) -> p m j e", j=ANGLES, e=2),
+                    in0=rotated[:, c, :].rearrange("p (m j e) -> p m j e", j=ANGLES, e=2)[:, :, :, ::-1],
+                    in1=sin_table[:, slot, :, :].unsqueeze(1).to_broadcast([P, 2 * HEADS, ANGLES, 2]),
+                    op=ALU.mult,
+                )
+            nc.scalar.copy(
+                out=out_sb[:, 0:2, first : first + PAIR, :, ROT:HEAD_DIM],
+                in_=others[:].rearrange("p c (k h i) -> p k c h i", k=2, h=HEADS),
+            )
+            nc.scalar.copy(
+                out=out_sb[:, 2, first : first + PAIR, :, :],
+                in_=values[:].rearrange("p c (h d) -> p c h d", h=HEADS),
+            )
+
+        def store(chunk, which):
+            batch, part = divmod(chunk, CHUNKS_PER_BATCH)
+            nc.sync.dma_start(
+                out=out_dram[which][batch, :, part * CHUNK : (part + 1) * CHUNK, :],
+                in_=out_of[chunk][:, which].rearrange("p c h d -> p c (h d)"),
+            )
+
+        def finish_chunk(chunk):
+            rotated_part = out_of[chunk][:, 0:2, :, :, 0:ROT]
+            nc.vector.tensor_tensor(
+                out=rotated_part,
+                in0=rotated_part,
+                in1=cross_of[chunk][:].rearrange("p c (k h i) -> p k c h i", k=2, h=HEADS),
+                op=ALU.add,
+            )
+            store(chunk, 0)
+            store(chunk, 1)
+
+        for step in range(N_PAIRS + 3):
+            if step < N_PAIRS:
+                transpose_pair(step)
+            if 1 <= step <= N_PAIRS:
+                project_pair(step - 1)
+            if 2 <= step <= N_PAIRS + 1:
+                finish_pair(step - 2)
+                if (step - 2) % (CHUNK // PAIR) == CHUNK // PAIR - 1:
+                    store((step - 2) * PAIR // CHUNK, 2)
+            if step >= 3 and (step - 3) % (CHUNK // PAIR) == CHUNK // PAIR - 1:
+                finish_chunk((step - 3) * PAIR // CHUNK)

@@ -18,6 +18,7 @@ BATCH, SEQ, EMBED = 4, 2048, 512
 HEADS, HEAD_DIM, ROT = 4, 64, 32
 WIDTH = HEADS * HEAD_DIM
 ANGLES = ROT // 2
+SPLIT = 8
 SLOTS = SEQ // P
 PAIR = 2
 CHUNK = 4
@@ -66,6 +67,7 @@ def tile_progenattention_pa_t_kernel(
         work = ctx.enter_context(tc.tile_pool(name="work", bufs=3))
         out_pool = ctx.enter_context(tc.tile_pool(name="out", bufs=8))
         psum = ctx.enter_context(tc.psum_pool(name="psum", bufs=2))
+        ctx.enter_context(tc.manual_schedule())
 
         x_tiles = []
 
@@ -94,19 +96,24 @@ def tile_progenattention_pa_t_kernel(
         nc.vector.memset(warm[:], 0.0)
         nc.scalar.activation(out=warm[:], in_=warm[:], func=ACT.Sin)
 
-        position_i = const.tile([P, SLOTS], I32)
-        nc.gpsimd.iota(position_i[:], pattern=[[1, SLOTS]], base=0, channel_multiplier=SLOTS)
+        position = const.tile([P, SLOTS], F32)
+        nc.gpsimd.iota(
+            position[:], pattern=[[1, SLOTS]], base=0, channel_multiplier=SLOTS,
+            allow_small_or_imprecise_dtypes=True,
+        )
         ident = const.tile([P, P], F32)
         make_identity(nc, ident[:])
-        position = const.tile([P, SLOTS], F32)
-        nc.vector.tensor_copy(out=position[:], in_=position_i[:])
 
         turns_high = const.tile([P, SLOTS, ANGLES], F32)
-        turns_low = const.tile([P, SLOTS, ANGLES], F32)
+        turns_low = const.tile([P, SLOTS, SPLIT], F32)
         for j in range(ANGLES):
-            high, low = split_constant(1.0 / (10000.0 ** (2 * j / ROT)) / TWO_PI)
+            turns_per_position = 1.0 / (10000.0 ** (2 * j / ROT)) / TWO_PI
+            if j < SPLIT:
+                high, low = split_constant(turns_per_position)
+                nc.vector.tensor_scalar_mul(out=turns_low[:, :, j], in0=position[:], scalar1=low)
+            else:
+                high = turns_per_position
             nc.vector.tensor_scalar_mul(out=turns_high[:, :, j], in0=position[:], scalar1=high)
-            nc.vector.tensor_scalar_mul(out=turns_low[:, :, j], in0=position[:], scalar1=low)
 
         def drop_whole_turns(name, turns):
             whole = const.tile([P, SLOTS, ANGLES], F32, name=name + "_whole")
@@ -119,27 +126,33 @@ def tile_progenattention_pa_t_kernel(
             return rest
 
         high_rest = drop_whole_turns("high_rest", turns_high)
-        turns = const.tile([P, SLOTS, ANGLES], F32)
-        nc.vector.tensor_tensor(out=turns[:], in0=high_rest[:], in1=turns_low[:], op=ALU.add)
-        sin_turns = drop_whole_turns("sin_turns", turns)
-        quarter_on = const.tile([P, SLOTS, ANGLES], F32)
-        nc.vector.tensor_scalar_add(out=quarter_on[:], in0=sin_turns[:], scalar1=0.25)
-        cos_turns = drop_whole_turns("cos_turns", quarter_on)
+        nc.vector.tensor_tensor(
+            out=high_rest[:, :, 0:SPLIT], in0=high_rest[:, :, 0:SPLIT], in1=turns_low[:], op=ALU.add
+        )
+        sin_turns = drop_whole_turns("sin_turns", high_rest)
+        abs_turns = const.tile([P, SLOTS, ANGLES], F32)
+        nc.vector.scalar_tensor_tensor(
+            out=abs_turns[:], in0=sin_turns[:], scalar=-1.0, in1=sin_turns[:],
+            op0=ALU.mult, op1=ALU.max,
+        )
 
         sin_table = const.tile([P, SLOTS, ANGLES, 2], F32)
         cos_table = const.tile([P, SLOTS, ROT], F32)
-        nc.scalar.activation(
-            out=sin_table[:, :, :, 0], in_=sin_turns[:], func=ACT.Sin, scale=-TWO_PI
-        )
-        nc.scalar.activation(
-            out=sin_table[:, :, :, 1], in_=sin_turns[:], func=ACT.Sin, scale=TWO_PI
-        )
-        nc.scalar.activation(
-            out=cos_table[:].rearrange("p t (j e) -> p t j e", e=2),
-            in_=cos_turns[:].unsqueeze(3).to_broadcast([P, SLOTS, ANGLES, 2]),
-            func=ACT.Sin,
-            scale=TWO_PI,
-        )
+
+        def make_tables():
+            nc.scalar.activation(
+                out=sin_table[:, :, :, 0], in_=sin_turns[:], func=ACT.Sin, scale=-TWO_PI
+            )
+            nc.scalar.activation(
+                out=sin_table[:, :, :, 1], in_=sin_turns[:], func=ACT.Sin, scale=TWO_PI
+            )
+            nc.scalar.activation(
+                out=cos_table[:].rearrange("p t (j e) -> p t j e", e=2),
+                in_=abs_turns[:].unsqueeze(3).to_broadcast([P, SLOTS, ANGLES, 2]),
+                func=ACT.Sin,
+                scale=-TWO_PI,
+                bias=TWO_PI / 4.0,
+            )
 
         w_words = const.tile([P, 2 * 3 * WIDTH], U8, align_bytes=64)
         w_scales = const.tile([P, 3 * WIDTH], U8, align_bytes=64)
@@ -242,6 +255,8 @@ def tile_progenattention_pa_t_kernel(
         for step in range(N_PAIRS + 3):
             if step < N_PAIRS:
                 transpose_pair(step)
+            if step == 1:
+                make_tables()
             if 1 <= step <= N_PAIRS:
                 project_pair(step - 1)
             if 2 <= step <= N_PAIRS + 1:

@@ -19,6 +19,7 @@ HEADS, HEAD_DIM, ROT = 4, 64, 32
 WIDTH = HEADS * HEAD_DIM
 ANGLES = ROT // 2
 SPLIT = 8
+WARM_UP = 3
 SLOTS = SEQ // P
 PAIR = 2
 CHUNK = 4
@@ -104,6 +105,10 @@ def tile_progenattention_pa_t_kernel(
         ident = const.tile([P, P], F32)
         make_identity(nc, ident[:])
 
+        warm_bank = psum.tile([P, P], F32, name="values")
+        for i in range(WARM_UP):
+            nc.tensor.matmul(out=warm_bank[:], lhsT=ident[:], rhs=ident[:], start=True, stop=True)
+
         turns_high = const.tile([P, SLOTS, ANGLES], F32)
         turns_low = const.tile([P, SLOTS, SPLIT], F32)
         for j in range(ANGLES):
@@ -139,13 +144,10 @@ def tile_progenattention_pa_t_kernel(
         sin_table = const.tile([P, SLOTS, ANGLES, 2], F32)
         cos_table = const.tile([P, SLOTS, ROT], F32)
 
-        def make_tables():
-            nc.scalar.activation(
-                out=sin_table[:, :, :, 0], in_=sin_turns[:], func=ACT.Sin, scale=-TWO_PI
-            )
-            nc.scalar.activation(
-                out=sin_table[:, :, :, 1], in_=sin_turns[:], func=ACT.Sin, scale=TWO_PI
-            )
+        sin_plain = const.tile([P, SLOTS, ANGLES], F32)
+
+        def sines_and_cosines():
+            nc.scalar.activation(out=sin_plain[:], in_=sin_turns[:], func=ACT.Sin, scale=TWO_PI)
             nc.scalar.activation(
                 out=cos_table[:].rearrange("p t (j e) -> p t j e", e=2),
                 in_=abs_turns[:].unsqueeze(3).to_broadcast([P, SLOTS, ANGLES, 2]),
@@ -153,6 +155,10 @@ def tile_progenattention_pa_t_kernel(
                 scale=-TWO_PI,
                 bias=TWO_PI / 4.0,
             )
+
+        def pair_up_sines():
+            nc.vector.tensor_scalar_mul(out=sin_table[:, :, :, 0], in0=sin_plain[:], scalar1=-1.0)
+            nc.vector.tensor_copy(out=sin_table[:, :, :, 1], in_=sin_plain[:])
 
         w_words = const.tile([P, 2 * 3 * WIDTH], U8, align_bytes=64)
         w_scales = const.tile([P, 3 * WIDTH], U8, align_bytes=64)
@@ -188,9 +194,9 @@ def tile_progenattention_pa_t_kernel(
             others = psum.tile([P, PAIR, WIDTH], F32)
             values = psum.tile([P, PAIR, WIDTH], F32)
             banks_of[pair] = (rotated, others, values)
-            for c in range(PAIR):
-                tokens = slice(c * P, (c + 1) * P)
-                for n, bank in enumerate(banks_of[pair]):
+            for n, bank in enumerate(banks_of[pair]):
+                for c in range(PAIR):
+                    tokens = slice(c * P, (c + 1) * P)
                     nc.tensor.matmul_mx(
                         out=bank[:, c, :],
                         lhsT=codes[:, tokens].bitcast(FP8X4),
@@ -252,16 +258,18 @@ def tile_progenattention_pa_t_kernel(
             store(chunk, 0)
             store(chunk, 1)
 
-        for step in range(N_PAIRS + 3):
+        for step in range(N_PAIRS + 5):
             if step < N_PAIRS:
                 transpose_pair(step)
-            if step == 1:
-                make_tables()
-            if 1 <= step <= N_PAIRS:
-                project_pair(step - 1)
-            if 2 <= step <= N_PAIRS + 1:
-                finish_pair(step - 2)
-                if (step - 2) % (CHUNK // PAIR) == CHUNK // PAIR - 1:
-                    store((step - 2) * PAIR // CHUNK, 2)
-            if step >= 3 and (step - 3) % (CHUNK // PAIR) == CHUNK // PAIR - 1:
-                finish_chunk((step - 3) * PAIR // CHUNK)
+            if step == 0:
+                sines_and_cosines()
+            if 0 <= step - 2 < N_PAIRS:
+                project_pair(step - 2)
+            if step == 2:
+                pair_up_sines()
+            if 0 <= step - 3 < N_PAIRS:
+                finish_pair(step - 3)
+                if (step - 3) % (CHUNK // PAIR) == CHUNK // PAIR - 1:
+                    store((step - 3) * PAIR // CHUNK, 2)
+            if step >= 4 and (step - 4) % (CHUNK // PAIR) == CHUNK // PAIR - 1:
+                finish_chunk((step - 4) * PAIR // CHUNK)

@@ -168,7 +168,7 @@ def tile_progenattention_pa_t_kernel(
         grouped_of = {}
         banks_of = {}
         out_of = {}
-        cross_of = {}
+        products_of = {}
 
         def transpose_pair(pair):
             chunk, first = divmod(pair * PAIR, CHUNK)
@@ -211,26 +211,32 @@ def tile_progenattention_pa_t_kernel(
             chunk, first = divmod(pair * PAIR, CHUNK)
             if first == 0:
                 out_sb = out_pool.tile([P, 3, CHUNK, HEADS, HEAD_DIM], F32)
+                direct = work.tile([P, CHUNK, 2 * HEADS * ROT], F32)
                 cross = work.tile([P, CHUNK, 2 * HEADS * ROT], F32)
                 out_of[chunk] = out_sb
-                cross_of[chunk] = cross
+                products_of[chunk] = (direct, cross)
             out_sb = out_of[chunk]
-            cross = cross_of[chunk]
+            direct, cross = products_of[chunk]
             rotated, others, values = banks_of[pair]
-            for c in range(PAIR):
-                slot = (chunk % CHUNKS_PER_BATCH) * CHUNK + first + c
-                nc.vector.tensor_tensor(
-                    out=out_sb[:, 0:2, first + c, :, 0:ROT],
-                    in0=rotated[:, c, :].rearrange("p (k h i) -> p k h i", k=2, h=HEADS),
-                    in1=cos_table[:, slot, :].unsqueeze(1).unsqueeze(1).to_broadcast([P, 2, HEADS, ROT]),
-                    op=ALU.mult,
-                )
-                nc.vector.tensor_tensor(
-                    out=cross[:, first + c, :].rearrange("p (m j e) -> p m j e", j=ANGLES, e=2),
-                    in0=rotated[:, c, :].rearrange("p (m j e) -> p m j e", j=ANGLES, e=2)[:, :, :, ::-1],
-                    in1=sin_table[:, slot, :, :].unsqueeze(1).to_broadcast([P, 2 * HEADS, ANGLES, 2]),
-                    op=ALU.mult,
-                )
+            slot = (chunk % CHUNKS_PER_BATCH) * CHUNK + first
+            nc.vector.tensor_tensor(
+                out=direct[:, first : first + PAIR, :].rearrange("p c (m i) -> p c m i", i=ROT),
+                in0=rotated[:].rearrange("p c (m i) -> p c m i", i=ROT),
+                in1=cos_table[:, slot : slot + PAIR, :]
+                .unsqueeze(2)
+                .to_broadcast([P, PAIR, 2 * HEADS, ROT]),
+                op=ALU.mult,
+            )
+            nc.vector.tensor_tensor(
+                out=cross[:, first : first + PAIR, :].rearrange(
+                    "p c (m j e) -> p c m j e", j=ANGLES, e=2
+                ),
+                in0=rotated[:].rearrange("p c (m j e) -> p c m j e", j=ANGLES, e=2)[:, :, :, :, ::-1],
+                in1=sin_table[:, slot : slot + PAIR, :, :]
+                .unsqueeze(2)
+                .to_broadcast([P, PAIR, 2 * HEADS, ANGLES, 2]),
+                op=ALU.mult,
+            )
             nc.scalar.copy(
                 out=out_sb[:, 0:2, first : first + PAIR, :, ROT:HEAD_DIM],
                 in_=others[:].rearrange("p c (k h i) -> p k c h i", k=2, h=HEADS),
@@ -248,11 +254,11 @@ def tile_progenattention_pa_t_kernel(
             )
 
         def finish_chunk(chunk):
-            rotated_part = out_of[chunk][:, 0:2, :, :, 0:ROT]
+            direct, cross = products_of[chunk]
             nc.vector.tensor_tensor(
-                out=rotated_part,
-                in0=rotated_part,
-                in1=cross_of[chunk][:].rearrange("p c (k h i) -> p k c h i", k=2, h=HEADS),
+                out=out_of[chunk][:, 0:2, :, :, 0:ROT],
+                in0=direct[:].rearrange("p c (k h i) -> p k c h i", k=2, h=HEADS),
+                in1=cross[:].rearrange("p c (k h i) -> p k c h i", k=2, h=HEADS),
                 op=ALU.add,
             )
             store(chunk, 0)

@@ -66,6 +66,7 @@ def tile_progenattention_pa_t_kernel(
         const = ctx.enter_context(tc.tile_pool(name="const", bufs=1))
         x_pool = ctx.enter_context(tc.tile_pool(name="x", bufs=N_CHUNKS))
         work = ctx.enter_context(tc.tile_pool(name="work", bufs=3))
+        products = ctx.enter_context(tc.tile_pool(name="products", bufs=4))
         out_pool = ctx.enter_context(tc.tile_pool(name="out", bufs=8))
         psum = ctx.enter_context(tc.psum_pool(name="psum", bufs=2))
         ctx.enter_context(tc.manual_schedule())
@@ -211,16 +212,15 @@ def tile_progenattention_pa_t_kernel(
             chunk, first = divmod(pair * PAIR, CHUNK)
             if first == 0:
                 out_sb = out_pool.tile([P, 3, CHUNK, HEADS, HEAD_DIM], F32)
-                direct = work.tile([P, CHUNK, 2 * HEADS * ROT], F32)
-                cross = work.tile([P, CHUNK, 2 * HEADS * ROT], F32)
                 out_of[chunk] = out_sb
-                products_of[chunk] = (direct, cross)
             out_sb = out_of[chunk]
-            direct, cross = products_of[chunk]
+            direct = products.tile([P, PAIR, 2 * HEADS * ROT], F32)
+            cross = products.tile([P, PAIR, 2 * HEADS * ROT], F32)
+            products_of[pair] = (direct, cross)
             rotated, others, values = banks_of[pair]
             slot = (chunk % CHUNKS_PER_BATCH) * CHUNK + first
             nc.vector.tensor_tensor(
-                out=direct[:, first : first + PAIR, :].rearrange("p c (m i) -> p c m i", i=ROT),
+                out=direct[:].rearrange("p c (m i) -> p c m i", i=ROT),
                 in0=rotated[:].rearrange("p c (m i) -> p c m i", i=ROT),
                 in1=cos_table[:, slot : slot + PAIR, :]
                 .unsqueeze(2)
@@ -228,9 +228,7 @@ def tile_progenattention_pa_t_kernel(
                 op=ALU.mult,
             )
             nc.vector.tensor_tensor(
-                out=cross[:, first : first + PAIR, :].rearrange(
-                    "p c (m j e) -> p c m j e", j=ANGLES, e=2
-                ),
+                out=cross[:].rearrange("p c (m j e) -> p c m j e", j=ANGLES, e=2),
                 in0=rotated[:].rearrange("p c (m j e) -> p c m j e", j=ANGLES, e=2)[:, :, :, :, ::-1],
                 in1=sin_table[:, slot : slot + PAIR, :, :]
                 .unsqueeze(2)
@@ -253,18 +251,21 @@ def tile_progenattention_pa_t_kernel(
                 in_=out_of[chunk][:, which].rearrange("p c h d -> p c (h d)"),
             )
 
-        def finish_chunk(chunk):
-            direct, cross = products_of[chunk]
-            nc.vector.tensor_tensor(
-                out=out_of[chunk][:, 0:2, :, :, 0:ROT],
+        def sum_pair(pair):
+            chunk, first = divmod(pair * PAIR, CHUNK)
+            engine = nc.vector if pair == N_PAIRS - 1 else nc.gpsimd
+            direct, cross = products_of[pair]
+            engine.tensor_tensor(
+                out=out_of[chunk][:, 0:2, first : first + PAIR, :, 0:ROT],
                 in0=direct[:].rearrange("p c (k h i) -> p k c h i", k=2, h=HEADS),
                 in1=cross[:].rearrange("p c (k h i) -> p k c h i", k=2, h=HEADS),
                 op=ALU.add,
             )
-            store(chunk, 0)
-            store(chunk, 1)
+            if first + PAIR == CHUNK:
+                store(chunk, 0)
+                store(chunk, 1)
 
-        for step in range(N_PAIRS + 5):
+        for step in range(N_PAIRS + 3):
             if step < N_PAIRS:
                 transpose_pair(step)
             if step == 0:
@@ -277,5 +278,4 @@ def tile_progenattention_pa_t_kernel(
                 finish_pair(step - 3)
                 if (step - 3) % (CHUNK // PAIR) == CHUNK // PAIR - 1:
                     store((step - 3) * PAIR // CHUNK, 2)
-            if step >= 4 and (step - 4) % (CHUNK // PAIR) == CHUNK // PAIR - 1:
-                finish_chunk((step - 4) * PAIR // CHUNK)
+                sum_pair(step - 3)

@@ -23,9 +23,11 @@ WARM_UP = 3
 SLOTS = SEQ // P
 PAIR = 2
 CHUNK = 4
-CHUNKS_PER_BATCH = SLOTS // CHUNK
-N_CHUNKS = BATCH * CHUNKS_PER_BATCH
-N_PAIRS = N_CHUNKS * CHUNK // PAIR
+N_TILES = BATCH * SLOTS
+N_PAIRS = N_TILES // PAIR
+STORE = 8
+LOADS = [CHUNK] * (SLOTS // CHUNK) + [SLOTS] * (BATCH - 1)
+STORES = [STORE] * (N_TILES // STORE - 1) + [CHUNK] * (STORE // CHUNK)
 TWO_PI = 6.283185307179586
 ROUND = 12582912.0
 
@@ -64,35 +66,36 @@ def tile_progenattention_pa_t_kernel(
 
     with ExitStack() as ctx:
         const = ctx.enter_context(tc.tile_pool(name="const", bufs=1))
-        x_pool = ctx.enter_context(tc.tile_pool(name="x", bufs=N_CHUNKS))
+        x_small = ctx.enter_context(tc.tile_pool(name="x_small", bufs=SLOTS // CHUNK))
+        x_large = ctx.enter_context(tc.tile_pool(name="x_large", bufs=BATCH - 1))
         work = ctx.enter_context(tc.tile_pool(name="work", bufs=3))
         products = ctx.enter_context(tc.tile_pool(name="products", bufs=4))
-        out_pool = ctx.enter_context(tc.tile_pool(name="out", bufs=8))
+        out_pool = ctx.enter_context(tc.tile_pool(name="out", bufs=4))
         psum = ctx.enter_context(tc.psum_pool(name="psum", bufs=2))
         ctx.enter_context(tc.manual_schedule())
 
-        x_tiles = []
+        x_of = {}
 
-        def load_chunk(chunk):
-            batch, part = divmod(chunk, CHUNKS_PER_BATCH)
-            x_sb = x_pool.tile([P, CHUNK, EMBED], BF16)
-            nc.sync.dma_start(
-                out=x_sb[:], in_=x_dram[batch, :, part * CHUNK : (part + 1) * CHUNK, :]
-            )
-            x_tiles.append(x_sb)
+        def load(first, count):
+            batch, slot = divmod(first, SLOTS)
+            pool = x_small if count == CHUNK else x_large
+            x_sb = pool.tile([P, count, EMBED], BF16)
+            nc.sync.dma_start(out=x_sb[:], in_=x_dram[batch, :, slot : slot + count, :])
+            for place in range(count):
+                x_of[first + place] = (x_sb, place)
 
         w_scales_in = const.tile([P, 3 * WIDTH], U8, align_bytes=64)
         nc.vector.memset(w_scales_in[:].bitcast(I32), 0)
         w_words_in = const.tile([P, 2 * 3 * WIDTH], U8, align_bytes=64)
-        load_chunk(0)
+        load(0, LOADS[0])
         for quadrant in range(4):
             nc.sync.dma_start(
                 out=w_scales_in[32 * quadrant : 32 * quadrant + 4, :].bitcast(I32),
                 in_=W_qkv_scales[0, 4 * quadrant : 4 * quadrant + 4, :].bitcast(I32),
             )
         nc.sync.dma_start(out=w_words_in[:].bitcast(I32), in_=W_qkv_words[0].bitcast(I32))
-        for chunk in range(1, N_CHUNKS):
-            load_chunk(chunk)
+        for n in range(1, len(LOADS)):
+            load(sum(LOADS[:n]), LOADS[n])
 
         warm = const.tile([P, 1], F32)
         nc.vector.memset(warm[:], 0.0)
@@ -172,10 +175,10 @@ def tile_progenattention_pa_t_kernel(
         products_of = {}
 
         def transpose_pair(pair):
-            chunk, first = divmod(pair * PAIR, CHUNK)
             flipped = psum.tile([P, PAIR, 2, P], F32)
             for c in range(PAIR):
-                words = x_tiles[chunk][:, first + c, :].bitcast(F32)
+                x_sb, place = x_of[pair * PAIR + c]
+                words = x_sb[:, place, :].bitcast(F32)
                 for odd in range(2):
                     nc.tensor.transpose(flipped[:, c, odd, :], words[:, odd : EMBED // 2 : 2], ident[:])
             grouped = work.tile([P, PAIR * P * 4], BF16, align_bytes=64)
@@ -208,17 +211,29 @@ def tile_progenattention_pa_t_kernel(
                         stop=True,
                     )
 
+        group_of = {}
+        for group in range(len(STORES)):
+            for place in range(STORES[group]):
+                group_of[sum(STORES[:group]) + place] = (group, place)
+
+        def store(group, which):
+            batch, slot = divmod(sum(STORES[:group]), SLOTS)
+            nc.sync.dma_start(
+                out=out_dram[which][batch, :, slot : slot + STORES[group], :],
+                in_=out_of[group][:, which].rearrange("p c h d -> p c (h d)"),
+            )
+
         def finish_pair(pair):
-            chunk, first = divmod(pair * PAIR, CHUNK)
-            if first == 0:
-                out_sb = out_pool.tile([P, 3, CHUNK, HEADS, HEAD_DIM], F32)
-                out_of[chunk] = out_sb
-            out_sb = out_of[chunk]
+            group, place = group_of[pair * PAIR]
+            if place == 0:
+                out_sb = out_pool.tile([P, 3, STORES[group], HEADS, HEAD_DIM], F32)
+                out_of[group] = out_sb
+            out_sb = out_of[group]
             direct = products.tile([P, PAIR, 2 * HEADS * ROT], F32)
             cross = products.tile([P, PAIR, 2 * HEADS * ROT], F32)
             products_of[pair] = (direct, cross)
             rotated, others, values = banks_of[pair]
-            slot = (chunk % CHUNKS_PER_BATCH) * CHUNK + first
+            slot = pair * PAIR % SLOTS
             nc.vector.tensor_tensor(
                 out=direct[:].rearrange("p c (m i) -> p c m i", i=ROT),
                 in0=rotated[:].rearrange("p c (m i) -> p c m i", i=ROT),
@@ -236,34 +251,29 @@ def tile_progenattention_pa_t_kernel(
                 op=ALU.mult,
             )
             nc.scalar.copy(
-                out=out_sb[:, 0:2, first : first + PAIR, :, ROT:HEAD_DIM],
+                out=out_sb[:, 0:2, place : place + PAIR, :, ROT:HEAD_DIM],
                 in_=others[:].rearrange("p c (k h i) -> p k c h i", k=2, h=HEADS),
             )
             nc.scalar.copy(
-                out=out_sb[:, 2, first : first + PAIR, :, :],
+                out=out_sb[:, 2, place : place + PAIR, :, :],
                 in_=values[:].rearrange("p c (h d) -> p c h d", h=HEADS),
             )
-
-        def store(chunk, which):
-            batch, part = divmod(chunk, CHUNKS_PER_BATCH)
-            nc.sync.dma_start(
-                out=out_dram[which][batch, :, part * CHUNK : (part + 1) * CHUNK, :],
-                in_=out_of[chunk][:, which].rearrange("p c h d -> p c (h d)"),
-            )
+            if place + PAIR == STORES[group]:
+                store(group, 2)
 
         def sum_pair(pair):
-            chunk, first = divmod(pair * PAIR, CHUNK)
+            group, place = group_of[pair * PAIR]
             engine = nc.vector if pair == N_PAIRS - 1 else nc.gpsimd
             direct, cross = products_of[pair]
             engine.tensor_tensor(
-                out=out_of[chunk][:, 0:2, first : first + PAIR, :, 0:ROT],
+                out=out_of[group][:, 0:2, place : place + PAIR, :, 0:ROT],
                 in0=direct[:].rearrange("p c (k h i) -> p k c h i", k=2, h=HEADS),
                 in1=cross[:].rearrange("p c (k h i) -> p k c h i", k=2, h=HEADS),
                 op=ALU.add,
             )
-            if first + PAIR == CHUNK:
-                store(chunk, 0)
-                store(chunk, 1)
+            if place + PAIR == STORES[group]:
+                store(group, 0)
+                store(group, 1)
 
         for step in range(N_PAIRS + 3):
             if step < N_PAIRS:
@@ -276,6 +286,4 @@ def tile_progenattention_pa_t_kernel(
                 pair_up_sines()
             if 0 <= step - 3 < N_PAIRS:
                 finish_pair(step - 3)
-                if (step - 3) % (CHUNK // PAIR) == CHUNK // PAIR - 1:
-                    store((step - 3) * PAIR // CHUNK, 2)
                 sum_pair(step - 3)

@@ -18,8 +18,6 @@ BATCH, SEQ, EMBED = 4, 2048, 512
 HEADS, HEAD_DIM, ROT = 4, 64, 32
 WIDTH = HEADS * HEAD_DIM
 ANGLES = ROT // 2
-SPLIT = 8
-WARM_UP = 3
 SLOTS = SEQ // P
 PAIR = 2
 CHUNK = 4
@@ -109,20 +107,12 @@ def tile_progenattention_pa_t_kernel(
         ident = const.tile([P, P], F32)
         make_identity(nc, ident[:])
 
-        warm_bank = psum.tile([P, P], F32, name="values")
-        for i in range(WARM_UP):
-            nc.tensor.matmul(out=warm_bank[:], lhsT=ident[:], rhs=ident[:], start=True, stop=True)
-
         turns_high = const.tile([P, SLOTS, ANGLES], F32)
-        turns_low = const.tile([P, SLOTS, SPLIT], F32)
+        turns_low = const.tile([P, SLOTS, ANGLES], F32)
         for j in range(ANGLES):
-            turns_per_position = 1.0 / (10000.0 ** (2 * j / ROT)) / TWO_PI
-            if j < SPLIT:
-                high, low = split_constant(turns_per_position)
-                nc.vector.tensor_scalar_mul(out=turns_low[:, :, j], in0=position[:], scalar1=low)
-            else:
-                high = turns_per_position
+            high, low = split_constant(1.0 / (10000.0 ** (2 * j / ROT)) / TWO_PI)
             nc.vector.tensor_scalar_mul(out=turns_high[:, :, j], in0=position[:], scalar1=high)
+            nc.vector.tensor_scalar_mul(out=turns_low[:, :, j], in0=position[:], scalar1=low)
 
         def drop_whole_turns(name, turns):
             whole = const.tile([P, SLOTS, ANGLES], F32, name=name + "_whole")
@@ -135,10 +125,9 @@ def tile_progenattention_pa_t_kernel(
             return rest
 
         high_rest = drop_whole_turns("high_rest", turns_high)
-        nc.vector.tensor_tensor(
-            out=high_rest[:, :, 0:SPLIT], in0=high_rest[:, :, 0:SPLIT], in1=turns_low[:], op=ALU.add
-        )
-        sin_turns = drop_whole_turns("sin_turns", high_rest)
+        turns = const.tile([P, SLOTS, ANGLES], F32)
+        nc.vector.tensor_tensor(out=turns[:], in0=high_rest[:], in1=turns_low[:], op=ALU.add)
+        sin_turns = drop_whole_turns("sin_turns", turns)
         abs_turns = const.tile([P, SLOTS, ANGLES], F32)
         nc.vector.scalar_tensor_tensor(
             out=abs_turns[:], in0=sin_turns[:], scalar=-1.0, in1=sin_turns[:],

@@ -21,11 +21,13 @@ ANGLES = ROT // 2
 SLOTS = SEQ // P
 PAIR = 2
 CHUNK = 4
-N_TILES = BATCH * SLOTS
-N_PAIRS = N_TILES // PAIR
-STORE = 8
-LOADS = [CHUNK] * (SLOTS // CHUNK) + [SLOTS] * (BATCH - 1)
-STORES = [STORE] * (N_TILES // STORE - 1) + [CHUNK] * (STORE // CHUNK)
+CHUNKS = SLOTS // CHUNK
+PAIRS = SLOTS // PAIR
+N_CHUNKS = BATCH * CHUNKS
+LOADS = [CHUNK, CHUNK, 2 * CHUNK] + [SLOTS] * (BATCH - 1)
+STORE_CHUNKS = [CHUNKS // 2] + [CHUNKS] * (BATCH - 1)
+VECTOR_SHARE = 4
+AHEAD = 1
 TWO_PI = 6.283185307179586
 ROUND = 12582912.0
 
@@ -64,20 +66,21 @@ def tile_progenattention_pa_t_kernel(
 
     with ExitStack() as ctx:
         const = ctx.enter_context(tc.tile_pool(name="const", bufs=1))
-        x_small = ctx.enter_context(tc.tile_pool(name="x_small", bufs=SLOTS // CHUNK))
-        x_large = ctx.enter_context(tc.tile_pool(name="x_large", bufs=BATCH - 1))
-        work = ctx.enter_context(tc.tile_pool(name="work", bufs=3))
-        products = ctx.enter_context(tc.tile_pool(name="products", bufs=4))
-        out_pool = ctx.enter_context(tc.tile_pool(name="out", bufs=4))
-        psum = ctx.enter_context(tc.psum_pool(name="psum", bufs=2))
+        x_pool = ctx.enter_context(tc.tile_pool(name="x", bufs=1))
+        grouped_pool = ctx.enter_context(tc.tile_pool(name="grouped", bufs=3))
+        codes_pool = ctx.enter_context(tc.tile_pool(name="codes", bufs=AHEAD + 3))
+        products = ctx.enter_context(tc.tile_pool(name="products", bufs=3))
+        out_pool = ctx.enter_context(tc.tile_pool(name="out", bufs=2))
+        flipped_pool = ctx.enter_context(tc.psum_pool(name="flipped", bufs=2))
+        banks = ctx.enter_context(tc.psum_pool(name="banks", bufs=6))
         ctx.enter_context(tc.manual_schedule())
 
         x_of = {}
 
-        def load(first, count):
+        def load(n):
+            first, count = sum(LOADS[:n]), LOADS[n]
             batch, slot = divmod(first, SLOTS)
-            pool = x_small if count == CHUNK else x_large
-            x_sb = pool.tile([P, count, EMBED], BF16)
+            x_sb = x_pool.tile([P, count, EMBED], BF16, name="x_%d" % n)
             nc.sync.dma_start(out=x_sb[:], in_=x_dram[batch, :, slot : slot + count, :])
             for place in range(count):
                 x_of[first + place] = (x_sb, place)
@@ -85,7 +88,7 @@ def tile_progenattention_pa_t_kernel(
         w_scales_in = const.tile([P, 3 * WIDTH], U8, align_bytes=64)
         nc.vector.memset(w_scales_in[:].bitcast(I32), 0)
         w_words_in = const.tile([P, 2 * 3 * WIDTH], U8, align_bytes=64)
-        load(0, LOADS[0])
+        load(0)
         for quadrant in range(4):
             nc.sync.dma_start(
                 out=w_scales_in[32 * quadrant : 32 * quadrant + 4, :].bitcast(I32),
@@ -93,7 +96,7 @@ def tile_progenattention_pa_t_kernel(
             )
         nc.sync.dma_start(out=w_words_in[:].bitcast(I32), in_=W_qkv_words[0].bitcast(I32))
         for n in range(1, len(LOADS)):
-            load(sum(LOADS[:n]), LOADS[n])
+            load(n)
 
         warm = const.tile([P, 1], F32)
         nc.vector.memset(warm[:], 0.0)
@@ -158,71 +161,84 @@ def tile_progenattention_pa_t_kernel(
         regroup_columns(nc, w_words[:].bitcast(I32), w_words_in[:].bitcast(I32))
         regroup_columns(nc, w_scales[:].bitcast(I32), w_scales_in[:].bitcast(I32))
 
+        flipped_of = {}
         grouped_of = {}
+        codes_of = {}
         banks_of = {}
-        out_of = {}
-        products_of = {}
+        v_of = {}
+        qk_of = {}
 
-        def transpose_pair(pair):
-            flipped = psum.tile([P, PAIR, 2, P], F32)
-            for c in range(PAIR):
-                x_sb, place = x_of[pair * PAIR + c]
-                words = x_sb[:, place, :].bitcast(F32)
-                for odd in range(2):
-                    nc.tensor.transpose(flipped[:, c, odd, :], words[:, odd : EMBED // 2 : 2], ident[:])
-            grouped = work.tile([P, PAIR * P * 4], BF16, align_bytes=64)
-            nc.scalar.copy(
-                out=grouped[:].bitcast(F32).rearrange("p (c r w) -> p c r w", c=PAIR, w=2),
-                in_=flipped[:].rearrange("p c w r -> p c r w"),
-            )
-            grouped_of[pair] = grouped
-
-        def project_pair(pair):
-            codes = work.tile([P, PAIR * P], U32, align_bytes=64)
-            scales = work.tile([P, PAIR * P], U8, align_bytes=64)
-            nc.vector.quantize_mx(
-                out=codes[:].bitcast(FP8X4), scales=scales[:], in_=grouped_of[pair][:]
-            )
-            rotated = psum.tile([P, PAIR, WIDTH], F32)
-            others = psum.tile([P, PAIR, WIDTH], F32)
-            values = psum.tile([P, PAIR, WIDTH], F32)
-            banks_of[pair] = (rotated, others, values)
-            for n, bank in enumerate(banks_of[pair]):
+        def transpose_chunk(chunk):
+            flipped_of[chunk] = []
+            for pair in range(CHUNK // PAIR):
+                flipped = flipped_pool.tile([P, PAIR, 2, P], F32, name="flipped", tag="flipped")
                 for c in range(PAIR):
-                    tokens = slice(c * P, (c + 1) * P)
-                    nc.tensor.matmul_mx(
-                        out=bank[:, c, :],
-                        lhsT=codes[:, tokens].bitcast(FP8X4),
-                        lhsT_scale=scales[:, tokens],
-                        rhs=w_words[:, 2 * n * WIDTH : 2 * (n + 1) * WIDTH].bitcast(FP4X4),
-                        rhs_scale=w_scales[:, n * WIDTH : (n + 1) * WIDTH],
-                        start=True,
-                        stop=True,
-                    )
+                    x_sb, place = x_of[chunk * CHUNK + pair * PAIR + c]
+                    words = x_sb[:, place, :].bitcast(F32)
+                    for odd in range(2):
+                        nc.tensor.transpose(
+                            flipped[:, c, odd, :], words[:, odd : EMBED // 2 : 2], ident[:]
+                        )
+                flipped_of[chunk].append(flipped)
 
-        group_of = {}
-        for group in range(len(STORES)):
-            for place in range(STORES[group]):
-                group_of[sum(STORES[:group]) + place] = (group, place)
+        def group_chunk(chunk):
+            grouped = grouped_pool.tile([P, CHUNK * P * 4], BF16, align_bytes=64)
+            words = grouped[:].bitcast(F32).rearrange("p (n c r w) -> p n c r w", n=2, c=PAIR, w=2)
+            for pair in range(CHUNK // PAIR):
+                nc.scalar.copy(
+                    out=words[:, pair], in_=flipped_of[chunk][pair][:].rearrange("p c w r -> p c r w")
+                )
+            grouped_of[chunk] = grouped
 
-        def store(group, which):
-            batch, slot = divmod(sum(STORES[:group]), SLOTS)
-            nc.sync.dma_start(
-                out=out_dram[which][batch, :, slot : slot + STORES[group], :],
-                in_=out_of[group][:, which].rearrange("p c h d -> p c (h d)"),
+        def quantize_chunk(chunk):
+            codes = codes_pool.tile([P, CHUNK * P], U32, align_bytes=64)
+            scales = codes_pool.tile([P, CHUNK * P], U8, align_bytes=64)
+            nc.vector.quantize_mx(
+                out=codes[:].bitcast(FP8X4), scales=scales[:], in_=grouped_of[chunk][:]
+            )
+            codes_of[chunk] = (codes, scales)
+
+        def project(pair, n):
+            bank = banks.tile([P, PAIR, WIDTH], F32, name="bank", tag="bank")
+            for c in range(PAIR):
+                tile = pair * PAIR + c
+                codes, scales = codes_of[tile // CHUNK]
+                tokens = slice(tile % CHUNK * P, (tile % CHUNK + 1) * P)
+                nc.tensor.matmul_mx(
+                    out=bank[:, c, :],
+                    lhsT=codes[:, tokens].bitcast(FP8X4),
+                    lhsT_scale=scales[:, tokens],
+                    rhs=w_words[:, 2 * n * WIDTH : 2 * (n + 1) * WIDTH].bitcast(FP4X4),
+                    rhs_scale=w_scales[:, n * WIDTH : (n + 1) * WIDTH],
+                    start=True,
+                    stop=True,
+                )
+            banks_of[pair, n] = bank
+
+        def copy_values(pair):
+            v_sb = v_of[pair // PAIRS]
+            place = pair % PAIRS * PAIR
+            out = v_sb[:, place : place + PAIR, :, :]
+            in_ = banks_of[pair, 2][:].rearrange("p c (h d) -> p c h d", h=HEADS)
+            if pair % VECTOR_SHARE == VECTOR_SHARE - 1:
+                nc.vector.tensor_copy(out=out, in_=in_)
+            else:
+                nc.scalar.copy(out=out, in_=in_)
+
+        def copy_others(pair):
+            qk_sb = qk_of[pair // PAIRS]
+            place = pair % PAIRS * PAIR
+            nc.scalar.copy(
+                out=qk_sb[:, :, place : place + PAIR, :, ROT:HEAD_DIM],
+                in_=banks_of[pair, 1][:].rearrange("p c (k h i) -> p k c h i", k=2, h=HEADS),
             )
 
-        def finish_pair(pair):
-            group, place = group_of[pair * PAIR]
-            if place == 0:
-                out_sb = out_pool.tile([P, 3, STORES[group], HEADS, HEAD_DIM], F32)
-                out_of[group] = out_sb
-            out_sb = out_of[group]
+        def rotate(pair):
+            qk_sb = qk_of[pair // PAIRS]
             direct = products.tile([P, PAIR, 2 * HEADS * ROT], F32)
             cross = products.tile([P, PAIR, 2 * HEADS * ROT], F32)
-            products_of[pair] = (direct, cross)
-            rotated, others, values = banks_of[pair]
-            slot = pair * PAIR % SLOTS
+            rotated = banks_of[pair, 0]
+            slot = pair % PAIRS * PAIR
             nc.vector.tensor_tensor(
                 out=direct[:].rearrange("p c (m i) -> p c m i", i=ROT),
                 in0=rotated[:].rearrange("p c (m i) -> p c m i", i=ROT),
@@ -239,40 +255,73 @@ def tile_progenattention_pa_t_kernel(
                 .to_broadcast([P, PAIR, 2 * HEADS, ANGLES, 2]),
                 op=ALU.mult,
             )
-            nc.scalar.copy(
-                out=out_sb[:, 0:2, place : place + PAIR, :, ROT:HEAD_DIM],
-                in_=others[:].rearrange("p c (k h i) -> p k c h i", k=2, h=HEADS),
-            )
-            nc.scalar.copy(
-                out=out_sb[:, 2, place : place + PAIR, :, :],
-                in_=values[:].rearrange("p c (h d) -> p c h d", h=HEADS),
-            )
-            if place + PAIR == STORES[group]:
-                store(group, 2)
-
-        def sum_pair(pair):
-            group, place = group_of[pair * PAIR]
-            engine = nc.vector if pair == N_PAIRS - 1 else nc.gpsimd
-            direct, cross = products_of[pair]
-            engine.tensor_tensor(
-                out=out_of[group][:, 0:2, place : place + PAIR, :, 0:ROT],
+            nc.gpsimd.tensor_tensor(
+                out=qk_sb[:, :, slot : slot + PAIR, :, 0:ROT],
                 in0=direct[:].rearrange("p c (k h i) -> p k c h i", k=2, h=HEADS),
                 in1=cross[:].rearrange("p c (k h i) -> p k c h i", k=2, h=HEADS),
                 op=ALU.add,
             )
-            if place + PAIR == STORES[group]:
-                store(group, 0)
-                store(group, 1)
 
-        for step in range(N_PAIRS + 3):
-            if step < N_PAIRS:
-                transpose_pair(step)
-            if step == 0:
-                sines_and_cosines()
-            if 0 <= step - 2 < N_PAIRS:
-                project_pair(step - 2)
-            if step == 2:
-                pair_up_sines()
-            if 0 <= step - 3 < N_PAIRS:
-                finish_pair(step - 3)
-                sum_pair(step - 3)
+        def store(which, chunk, rows):
+            batch, place = divmod(chunk, CHUNKS)
+            count = STORE_CHUNKS[batch]
+            if (place + 1) % count == 0:
+                tiles = slice((place + 1 - count) * CHUNK, (place + 1) * CHUNK)
+                nc.sync.dma_start(
+                    out=out_dram[which][batch, :, tiles, :],
+                    in_=rows[:, tiles].rearrange("p c h d -> p c (h d)"),
+                )
+
+        def pairs_of(chunk):
+            return range(chunk * CHUNK // PAIR, (chunk + 1) * CHUNK // PAIR)
+
+        def open_values(chunk):
+            if chunk % CHUNKS == 0:
+                v_sb = out_pool.tile([P, SLOTS, HEADS, HEAD_DIM], F32)
+                v_of[chunk // CHUNKS] = v_sb
+
+        for chunk in range(AHEAD + 1):
+            transpose_chunk(chunk)
+            group_chunk(chunk)
+        sines_and_cosines()
+        for chunk in range(AHEAD):
+            quantize_chunk(chunk)
+            open_values(chunk)
+            for pair in pairs_of(chunk):
+                project(pair, 2)
+            transpose_chunk(chunk + AHEAD + 1)
+            for pair in pairs_of(chunk):
+                copy_values(pair)
+            group_chunk(chunk + AHEAD + 1)
+        quantize_chunk(AHEAD)
+        pair_up_sines()
+
+        for step in range(N_CHUNKS):
+            batch = step // CHUNKS
+            values = step + AHEAD
+            if step % CHUNKS == 0:
+                qk_sb = out_pool.tile([P, 2, SLOTS, HEADS, HEAD_DIM], F32)
+                qk_of[batch] = qk_sb
+            if values < N_CHUNKS:
+                open_values(values)
+            for pair in pairs_of(step):
+                project(pair, 0)
+                project(pair, 1)
+                if values < N_CHUNKS:
+                    project(pair + AHEAD * CHUNK // PAIR, 2)
+            if values + 2 < N_CHUNKS:
+                transpose_chunk(values + 2)
+            for pair in pairs_of(step):
+                rotate(pair)
+            if values + 1 < N_CHUNKS:
+                quantize_chunk(values + 1)
+            for pair in pairs_of(step):
+                copy_others(pair)
+                if values < N_CHUNKS:
+                    copy_values(pair + AHEAD * CHUNK // PAIR)
+            if values < N_CHUNKS:
+                store(2, values, v_of[values // CHUNKS])
+            if values + 2 < N_CHUNKS:
+                group_chunk(values + 2)
+            store(0, step, qk_of[batch][:, 0])
+            store(1, step, qk_of[batch][:, 1])

@@ -22,12 +22,14 @@ SLOTS = SEQ // P
 PAIR = 2
 CHUNK = 4
 CHUNKS = SLOTS // CHUNK
-PAIRS = SLOTS // PAIR
 N_CHUNKS = BATCH * CHUNKS
+PAIRS = CHUNK // PAIR
+HALF = HEADS * ROT
 LOADS = [CHUNK, CHUNK, 2 * CHUNK] + [SLOTS] * (BATCH - 1)
-STORE_CHUNKS = [CHUNKS // 2] + [CHUNKS] * (BATCH - 1)
-VECTOR_SHARE = 4
-AHEAD = 1
+Q, K, V = range(3)
+AHEAD = {Q: 1, K: 0, V: 2}
+WHOLE = [CHUNKS]
+HALVES = [CHUNKS // 2, CHUNKS // 2]
 TWO_PI = 6.283185307179586
 ROUND = 12582912.0
 
@@ -44,17 +46,13 @@ def split_constant(value):
 
 def regroup_columns(nc, dst, src):
     natural = src.rearrange("p (g k s f w) -> p g k s f w", g=2, k=3, s=2, f=2)
-    blocks = dst.rearrange("p (n c) -> p n c", n=6)
-    for half in range(2):
-        for kind in range(2):
-            nc.vector.tensor_copy(
-                out=blocks[:, 2 * half + kind, :].rearrange("p (g s w) -> p g s w", g=2, s=2),
+    blocks = dst.rearrange("p (n c) -> p n c", n=4)
+    for kind in range(2):
+        for half in range(2):
+            nc.gpsimd.tensor_copy(
+                out=blocks[:, 2 * kind + half, :].rearrange("p (g s w) -> p g s w", g=2, s=2),
                 in_=natural[:, :, kind, :, half, :],
             )
-    nc.vector.tensor_copy(
-        out=blocks[:, 4:6, :],
-        in_=src.rearrange("p (g k c) -> p g k c", g=2, k=3)[:, :, 2, :],
-    )
 
 
 def tile_progenattention_pa_t_kernel(
@@ -68,8 +66,8 @@ def tile_progenattention_pa_t_kernel(
         const = ctx.enter_context(tc.tile_pool(name="const", bufs=1))
         x_pool = ctx.enter_context(tc.tile_pool(name="x", bufs=1))
         grouped_pool = ctx.enter_context(tc.tile_pool(name="grouped", bufs=3))
-        codes_pool = ctx.enter_context(tc.tile_pool(name="codes", bufs=AHEAD + 3))
-        products = ctx.enter_context(tc.tile_pool(name="products", bufs=3))
+        codes_pool = ctx.enter_context(tc.tile_pool(name="codes", bufs=5))
+        products = ctx.enter_context(tc.tile_pool(name="products", bufs=4))
         out_pool = ctx.enter_context(tc.tile_pool(name="out", bufs=2))
         flipped_pool = ctx.enter_context(tc.psum_pool(name="flipped", bufs=2))
         banks = ctx.enter_context(tc.psum_pool(name="banks", bufs=6))
@@ -156,8 +154,8 @@ def tile_progenattention_pa_t_kernel(
             nc.vector.tensor_scalar_mul(out=sin_table[:, :, :, 0], in0=sin_plain[:], scalar1=-1.0)
             nc.vector.tensor_copy(out=sin_table[:, :, :, 1], in_=sin_plain[:])
 
-        w_words = const.tile([P, 2 * 3 * WIDTH], U8, align_bytes=64)
-        w_scales = const.tile([P, 3 * WIDTH], U8, align_bytes=64)
+        w_words = const.tile([P, 2 * 2 * WIDTH], U8, align_bytes=64)
+        w_scales = const.tile([P, 2 * WIDTH], U8, align_bytes=64)
         regroup_columns(nc, w_words[:].bitcast(I32), w_words_in[:].bitcast(I32))
         regroup_columns(nc, w_scales[:].bitcast(I32), w_scales_in[:].bitcast(I32))
 
@@ -165,8 +163,7 @@ def tile_progenattention_pa_t_kernel(
         grouped_of = {}
         codes_of = {}
         banks_of = {}
-        v_of = {}
-        qk_of = {}
+        out_of = {}
 
         def transpose_chunk(chunk):
             flipped_of[chunk] = []
@@ -198,130 +195,135 @@ def tile_progenattention_pa_t_kernel(
             )
             codes_of[chunk] = (codes, scales)
 
-        def project(pair, n):
-            bank = banks.tile([P, PAIR, WIDTH], F32, name="bank", tag="bank")
-            for c in range(PAIR):
-                tile = pair * PAIR + c
-                codes, scales = codes_of[tile // CHUNK]
-                tokens = slice(tile % CHUNK * P, (tile % CHUNK + 1) * P)
-                nc.tensor.matmul_mx(
-                    out=bank[:, c, :],
-                    lhsT=codes[:, tokens].bitcast(FP8X4),
-                    lhsT_scale=scales[:, tokens],
-                    rhs=w_words[:, 2 * n * WIDTH : 2 * (n + 1) * WIDTH].bitcast(FP4X4),
-                    rhs_scale=w_scales[:, n * WIDTH : (n + 1) * WIDTH],
-                    start=True,
-                    stop=True,
-                )
-            banks_of[pair, n] = bank
-
-        def copy_values(pair):
-            v_sb = v_of[pair // PAIRS]
-            place = pair % PAIRS * PAIR
-            out = v_sb[:, place : place + PAIR, :, :]
-            in_ = banks_of[pair, 2][:].rearrange("p c (h d) -> p c h d", h=HEADS)
-            if pair % VECTOR_SHARE == VECTOR_SHARE - 1:
-                nc.vector.tensor_copy(out=out, in_=in_)
-            else:
-                nc.scalar.copy(out=out, in_=in_)
-
-        def copy_others(pair):
-            qk_sb = qk_of[pair // PAIRS]
-            place = pair % PAIRS * PAIR
-            nc.scalar.copy(
-                out=qk_sb[:, :, place : place + PAIR, :, ROT:HEAD_DIM],
-                in_=banks_of[pair, 1][:].rearrange("p c (k h i) -> p k c h i", k=2, h=HEADS),
+        def multiply(out, tile, words, scales, first):
+            codes, code_scales = codes_of[tile // CHUNK]
+            tokens = slice(tile % CHUNK * P, (tile % CHUNK + 1) * P)
+            nc.tensor.matmul_mx(
+                out=out,
+                lhsT=codes[:, tokens].bitcast(FP8X4),
+                lhsT_scale=code_scales[:, tokens],
+                rhs=words[:, 2 * first : 2 * (first + HALF)].bitcast(FP4X4),
+                rhs_scale=scales[:, first : first + HALF],
+                start=True,
+                stop=True,
             )
 
-        def rotate(pair):
-            qk_sb = qk_of[pair // PAIRS]
-            direct = products.tile([P, PAIR, 2 * HEADS * ROT], F32)
-            cross = products.tile([P, PAIR, 2 * HEADS * ROT], F32)
-            rotated = banks_of[pair, 0]
-            slot = pair % PAIRS * PAIR
+        def open_output(which, chunk):
+            if chunk % CHUNKS == 0:
+                out_sb = out_pool.tile(
+                    [P, SLOTS, HEADS, HEAD_DIM], F32, name="out_%d" % which, tag="out_%d" % which
+                )
+                out_of[which, chunk // CHUNKS] = out_sb
+
+        def project(which, chunk):
+            open_output(which, chunk)
+            for half in range(2):
+                bank = banks.tile([P, CHUNK, HALF], F32, name="bank", tag="bank")
+                for c in range(CHUNK):
+                    multiply(
+                        bank[:, c, :], chunk * CHUNK + c, w_words, w_scales, (2 * which + half) * HALF
+                    )
+                banks_of[which, chunk, half] = bank
+
+        def project_values(chunk):
+            open_output(V, chunk)
+            for pair in range(PAIRS):
+                bank = banks.tile([P, PAIR, WIDTH], F32, name="bank", tag="bank")
+                for c in range(PAIR):
+                    for group in range(2):
+                        multiply(
+                            bank[:, c, group * HALF : (group + 1) * HALF],
+                            chunk * CHUNK + pair * PAIR + c,
+                            w_words_in,
+                            w_scales_in,
+                            (3 * group + 2) * HALF,
+                        )
+                banks_of[V, chunk, pair] = bank
+
+        def copy_values(chunk):
+            for pair in range(PAIRS):
+                place = chunk % CHUNKS * CHUNK + pair * PAIR
+                nc.scalar.copy(
+                    out=out_of[V, chunk // CHUNKS][:, place : place + PAIR, :, :],
+                    in_=banks_of[V, chunk, pair][:].rearrange("p c (h d) -> p c h d", h=HEADS),
+                )
+
+        def copy_others(which, chunk):
+            place = chunk % CHUNKS * CHUNK
+            nc.scalar.copy(
+                out=out_of[which, chunk // CHUNKS][:, place : place + CHUNK, :, ROT:HEAD_DIM],
+                in_=banks_of[which, chunk, 1][:].rearrange("p c (h i) -> p c h i", h=HEADS),
+            )
+
+        def rotate(which, chunk):
+            direct = products.tile([P, CHUNK, HALF], F32)
+            cross = products.tile([P, CHUNK, HALF], F32)
+            rotated = banks_of[which, chunk, 0]
+            place = chunk % CHUNKS * CHUNK
             nc.vector.tensor_tensor(
-                out=direct[:].rearrange("p c (m i) -> p c m i", i=ROT),
-                in0=rotated[:].rearrange("p c (m i) -> p c m i", i=ROT),
-                in1=cos_table[:, slot : slot + PAIR, :]
+                out=direct[:].rearrange("p c (h i) -> p c h i", i=ROT),
+                in0=rotated[:].rearrange("p c (h i) -> p c h i", i=ROT),
+                in1=cos_table[:, place : place + CHUNK, :]
                 .unsqueeze(2)
-                .to_broadcast([P, PAIR, 2 * HEADS, ROT]),
+                .to_broadcast([P, CHUNK, HEADS, ROT]),
                 op=ALU.mult,
             )
             nc.vector.tensor_tensor(
-                out=cross[:].rearrange("p c (m j e) -> p c m j e", j=ANGLES, e=2),
-                in0=rotated[:].rearrange("p c (m j e) -> p c m j e", j=ANGLES, e=2)[:, :, :, :, ::-1],
-                in1=sin_table[:, slot : slot + PAIR, :, :]
+                out=cross[:].rearrange("p c (h j e) -> p c h j e", j=ANGLES, e=2),
+                in0=rotated[:].rearrange("p c (h j e) -> p c h j e", j=ANGLES, e=2)[:, :, :, :, ::-1],
+                in1=sin_table[:, place : place + CHUNK, :, :]
                 .unsqueeze(2)
-                .to_broadcast([P, PAIR, 2 * HEADS, ANGLES, 2]),
+                .to_broadcast([P, CHUNK, HEADS, ANGLES, 2]),
                 op=ALU.mult,
             )
             nc.gpsimd.tensor_tensor(
-                out=qk_sb[:, :, slot : slot + PAIR, :, 0:ROT],
-                in0=direct[:].rearrange("p c (k h i) -> p k c h i", k=2, h=HEADS),
-                in1=cross[:].rearrange("p c (k h i) -> p k c h i", k=2, h=HEADS),
+                out=out_of[which, chunk // CHUNKS][:, place : place + CHUNK, :, 0:ROT],
+                in0=direct[:].rearrange("p c (h i) -> p c h i", h=HEADS),
+                in1=cross[:].rearrange("p c (h i) -> p c h i", h=HEADS),
                 op=ALU.add,
             )
 
-        def store(which, chunk, rows):
+        def store(which, chunk):
             batch, place = divmod(chunk, CHUNKS)
-            count = STORE_CHUNKS[batch]
-            if (place + 1) % count == 0:
-                tiles = slice((place + 1 - count) * CHUNK, (place + 1) * CHUNK)
-                nc.sync.dma_start(
-                    out=out_dram[which][batch, :, tiles, :],
-                    in_=rows[:, tiles].rearrange("p c h d -> p c (h d)"),
-                )
+            end = 0
+            for count in HALVES if which == V and batch < BATCH // 2 else WHOLE:
+                end += count
+                if place + 1 == end:
+                    tiles = slice((end - count) * CHUNK, end * CHUNK)
+                    nc.sync.dma_start(
+                        out=out_dram[which][batch, :, tiles, :],
+                        in_=out_of[which, batch][:, tiles].rearrange("p c h d -> p c (h d)"),
+                    )
 
-        def pairs_of(chunk):
-            return range(chunk * CHUNK // PAIR, (chunk + 1) * CHUNK // PAIR)
+        transpose_chunk(0)
+        group_chunk(0)
+        quantize_chunk(0)
+        transpose_chunk(1)
+        for step in range(-AHEAD[V], N_CHUNKS):
+            chunk_of = {}
+            for which in (Q, K, V):
+                if 0 <= step + AHEAD[which] < N_CHUNKS:
+                    chunk_of[which] = step + AHEAD[which]
+            rotating = [which for which in (Q, K) if which in chunk_of]
 
-        def open_values(chunk):
-            if chunk % CHUNKS == 0:
-                v_sb = out_pool.tile([P, SLOTS, HEADS, HEAD_DIM], F32)
-                v_of[chunk // CHUNKS] = v_sb
-
-        for chunk in range(AHEAD + 1):
-            transpose_chunk(chunk)
-            group_chunk(chunk)
-        sines_and_cosines()
-        for chunk in range(AHEAD):
-            quantize_chunk(chunk)
-            open_values(chunk)
-            for pair in pairs_of(chunk):
-                project(pair, 2)
-            transpose_chunk(chunk + AHEAD + 1)
-            for pair in pairs_of(chunk):
-                copy_values(pair)
-            group_chunk(chunk + AHEAD + 1)
-        quantize_chunk(AHEAD)
-        pair_up_sines()
-
-        for step in range(N_CHUNKS):
-            batch = step // CHUNKS
-            values = step + AHEAD
-            if step % CHUNKS == 0:
-                qk_sb = out_pool.tile([P, 2, SLOTS, HEADS, HEAD_DIM], F32)
-                qk_of[batch] = qk_sb
-            if values < N_CHUNKS:
-                open_values(values)
-            for pair in pairs_of(step):
-                project(pair, 0)
-                project(pair, 1)
-                if values < N_CHUNKS:
-                    project(pair + AHEAD * CHUNK // PAIR, 2)
-            if values + 2 < N_CHUNKS:
-                transpose_chunk(values + 2)
-            for pair in pairs_of(step):
-                rotate(pair)
-            if values + 1 < N_CHUNKS:
-                quantize_chunk(values + 1)
-            for pair in pairs_of(step):
-                copy_others(pair)
-                if values < N_CHUNKS:
-                    copy_values(pair + AHEAD * CHUNK // PAIR)
-            if values < N_CHUNKS:
-                store(2, values, v_of[values // CHUNKS])
-            if values + 2 < N_CHUNKS:
-                group_chunk(values + 2)
-            store(0, step, qk_of[batch][:, 0])
-            store(1, step, qk_of[batch][:, 1])
+            for which in rotating:
+                project(which, chunk_of[which])
+            if V in chunk_of:
+                project_values(chunk_of[V])
+            if step + 4 < N_CHUNKS:
+                transpose_chunk(step + 4)
+            if step + 3 < N_CHUNKS:
+                group_chunk(step + 3)
+            if step == -AHEAD[V]:
+                sines_and_cosines()
+            for which in rotating:
+                rotate(which, chunk_of[which])
+                copy_others(which, chunk_of[which])
+            if V in chunk_of:
+                copy_values(chunk_of[V])
+            if step + 3 < N_CHUNKS:
+                quantize_chunk(step + 3)
+            if step == -AHEAD[V]:
+                pair_up_sines()
+            for which in chunk_of:
+                store(which, chunk_of[which])

@@ -286,7 +286,7 @@ def tile_progenattention_pa_t_kernel(
         def store(which, chunk):
             batch, place = divmod(chunk, CHUNKS)
             end = 0
-            for count in HALVES if which == V and batch < BATCH // 2 else WHOLE:
+            for count in HALVES if which == V and batch < BATCH - 1 else WHOLE:
                 end += count
                 if place + 1 == end:
                     tiles = slice((end - count) * CHUNK, end * CHUNK)

@@ -25,11 +25,17 @@ CHUNKS = SLOTS // CHUNK
 N_CHUNKS = BATCH * CHUNKS
 PAIRS = CHUNK // PAIR
 HALF = HEADS * ROT
-LOADS = [CHUNK, CHUNK, 2 * CHUNK] + [SLOTS] * (BATCH - 1)
+LOADS = [CHUNK, CHUNK, 2 * CHUNK, SLOTS, 2 * SLOTS]
 Q, K, V = range(3)
 AHEAD = {Q: 1, K: 0, V: 2}
 WHOLE = [CHUNKS]
 HALVES = [CHUNKS // 2, CHUNKS // 2]
+STORE_CHUNKS = {
+    Q: [WHOLE] * BATCH,
+    K: [WHOLE] * BATCH,
+    V: [HALVES] * 2 + [WHOLE] * (BATCH - 2),
+}
+VECTOR_SHARE = 4
 TWO_PI = 6.283185307179586
 ROUND = 12582912.0
 
@@ -45,8 +51,12 @@ def split_constant(value):
 
 
 def regroup_columns(nc, dst, src):
+    blocks = dst.rearrange("p (n c) -> p n c", n=6)
+    nc.gpsimd.tensor_copy(
+        out=blocks[:, 4:6, :],
+        in_=src.rearrange("p (g k c) -> p g k c", g=2, k=3)[:, :, 2, :],
+    )
     natural = src.rearrange("p (g k s f w) -> p g k s f w", g=2, k=3, s=2, f=2)
-    blocks = dst.rearrange("p (n c) -> p n c", n=4)
     for kind in range(2):
         for half in range(2):
             nc.gpsimd.tensor_copy(
@@ -78,8 +88,14 @@ def tile_progenattention_pa_t_kernel(
         def load(n):
             first, count = sum(LOADS[:n]), LOADS[n]
             batch, slot = divmod(first, SLOTS)
+            whole = max(count // SLOTS, 1)
             x_sb = x_pool.tile([P, count, EMBED], BF16, name="x_%d" % n)
-            nc.sync.dma_start(out=x_sb[:], in_=x_dram[batch, :, slot : slot + count, :])
+            nc.sync.dma_start(
+                out=x_sb[:].rearrange("p (b t) e -> p b t e", b=whole),
+                in_=x_dram[batch : batch + whole, :, slot : slot + count // whole, :].rearrange(
+                    "b p t e -> p b t e"
+                ),
+            )
             for place in range(count):
                 x_of[first + place] = (x_sb, place)
 
@@ -154,10 +170,13 @@ def tile_progenattention_pa_t_kernel(
             nc.vector.tensor_scalar_mul(out=sin_table[:, :, :, 0], in0=sin_plain[:], scalar1=-1.0)
             nc.vector.tensor_copy(out=sin_table[:, :, :, 1], in_=sin_plain[:])
 
-        w_words = const.tile([P, 2 * 2 * WIDTH], U8, align_bytes=64)
-        w_scales = const.tile([P, 2 * WIDTH], U8, align_bytes=64)
-        regroup_columns(nc, w_words[:].bitcast(I32), w_words_in[:].bitcast(I32))
+        w_words = const.tile([P, 2 * 3 * WIDTH], U8, align_bytes=64)
+        w_scales = const.tile([P, 3 * WIDTH], U8, align_bytes=64)
         regroup_columns(nc, w_scales[:].bitcast(I32), w_scales_in[:].bitcast(I32))
+        regroup_columns(nc, w_words[:].bitcast(I32), w_words_in[:].bitcast(I32))
+
+        ones = const.tile([P, 1], F32)
+        nc.gpsimd.memset(ones[:], 1.0)
 
         flipped_of = {}
         grouped_of = {}
@@ -195,15 +214,15 @@ def tile_progenattention_pa_t_kernel(
             )
             codes_of[chunk] = (codes, scales)
 
-        def multiply(out, tile, words, scales, first):
+        def multiply(out, tile, columns):
             codes, code_scales = codes_of[tile // CHUNK]
             tokens = slice(tile % CHUNK * P, (tile % CHUNK + 1) * P)
             nc.tensor.matmul_mx(
                 out=out,
                 lhsT=codes[:, tokens].bitcast(FP8X4),
                 lhsT_scale=code_scales[:, tokens],
-                rhs=words[:, 2 * first : 2 * (first + HALF)].bitcast(FP4X4),
-                rhs_scale=scales[:, first : first + HALF],
+                rhs=w_words[:, 2 * columns.start : 2 * columns.stop].bitcast(FP4X4),
+                rhs_scale=w_scales[:, columns],
                 start=True,
                 stop=True,
             )
@@ -219,10 +238,9 @@ def tile_progenattention_pa_t_kernel(
             open_output(which, chunk)
             for half in range(2):
                 bank = banks.tile([P, CHUNK, HALF], F32, name="bank", tag="bank")
+                first = (2 * which + half) * HALF
                 for c in range(CHUNK):
-                    multiply(
-                        bank[:, c, :], chunk * CHUNK + c, w_words, w_scales, (2 * which + half) * HALF
-                    )
+                    multiply(bank[:, c, :], chunk * CHUNK + c, slice(first, first + HALF))
                 banks_of[which, chunk, half] = bank
 
         def project_values(chunk):
@@ -230,14 +248,11 @@ def tile_progenattention_pa_t_kernel(
             for pair in range(PAIRS):
                 bank = banks.tile([P, PAIR, WIDTH], F32, name="bank", tag="bank")
                 for c in range(PAIR):
-                    for group in range(2):
-                        multiply(
-                            bank[:, c, group * HALF : (group + 1) * HALF],
-                            chunk * CHUNK + pair * PAIR + c,
-                            w_words_in,
-                            w_scales_in,
-                            (3 * group + 2) * HALF,
-                        )
+                    multiply(
+                        bank[:, c, :],
+                        chunk * CHUNK + pair * PAIR + c,
+                        slice(2 * WIDTH, 3 * WIDTH),
+                    )
                 banks_of[V, chunk, pair] = bank
 
         def copy_values(chunk):
@@ -248,12 +263,22 @@ def tile_progenattention_pa_t_kernel(
                     in_=banks_of[V, chunk, pair][:].rearrange("p c (h d) -> p c h d", h=HEADS),
                 )
 
+        def is_vectors(which, chunk):
+            return which == K and chunk % VECTOR_SHARE == VECTOR_SHARE - 1
+
         def copy_others(which, chunk):
             place = chunk % CHUNKS * CHUNK
-            nc.scalar.copy(
-                out=out_of[which, chunk // CHUNKS][:, place : place + CHUNK, :, ROT:HEAD_DIM],
-                in_=banks_of[which, chunk, 1][:].rearrange("p c (h i) -> p c h i", h=HEADS),
-            )
+            out = out_of[which, chunk // CHUNKS][:, place : place + CHUNK, :, ROT:HEAD_DIM]
+            in_ = banks_of[which, chunk, 1][:].rearrange("p c (h i) -> p c h i", h=HEADS)
+            if is_vectors(which, chunk):
+                nc.vector.tensor_tensor(
+                    out=out,
+                    in0=in_,
+                    in1=ones[:].unsqueeze(2).unsqueeze(3).to_broadcast([P, CHUNK, HEADS, ROT]),
+                    op=ALU.mult,
+                )
+            else:
+                nc.scalar.copy(out=out, in_=in_)
 
         def rotate(which, chunk):
             direct = products.tile([P, CHUNK, HALF], F32)
@@ -286,7 +311,7 @@ def tile_progenattention_pa_t_kernel(
         def store(which, chunk):
             batch, place = divmod(chunk, CHUNKS)
             end = 0
-            for count in HALVES if which == V and batch < BATCH - 1 else WHOLE:
+            for count in STORE_CHUNKS[which][batch]:
                 end += count
                 if place + 1 == end:
                     tiles = slice((end - count) * CHUNK, end * CHUNK)
@@ -318,11 +343,15 @@ def tile_progenattention_pa_t_kernel(
                 sines_and_cosines()
             for which in rotating:
                 rotate(which, chunk_of[which])
-                copy_others(which, chunk_of[which])
+                if not is_vectors(which, chunk_of[which]):
+                    copy_others(which, chunk_of[which])
             if V in chunk_of:
                 copy_values(chunk_of[V])
             if step + 3 < N_CHUNKS:
                 quantize_chunk(step + 3)
+            for which in rotating:
+                if is_vectors(which, chunk_of[which]):
+                    copy_others(which, chunk_of[which])
             if step == -AHEAD[V]:
                 pair_up_sines()
             for which in chunk_of:

@@ -30,12 +30,7 @@ Q, K, V = range(3)
 AHEAD = {Q: 1, K: 0, V: 2}
 WHOLE = [CHUNKS]
 HALVES = [CHUNKS // 2, CHUNKS // 2]
-STORE_CHUNKS = {
-    Q: [WHOLE] * BATCH,
-    K: [WHOLE] * BATCH,
-    V: [HALVES] * 2 + [WHOLE] * (BATCH - 2),
-}
-VECTOR_SHARE = 4
+STORE_CHUNKS = {Q: WHOLE, K: WHOLE, V: HALVES}
 TWO_PI = 6.283185307179586
 ROUND = 12582912.0
 
@@ -175,9 +170,6 @@ def tile_progenattention_pa_t_kernel(
         regroup_columns(nc, w_scales[:].bitcast(I32), w_scales_in[:].bitcast(I32))
         regroup_columns(nc, w_words[:].bitcast(I32), w_words_in[:].bitcast(I32))
 
-        ones = const.tile([P, 1], F32)
-        nc.gpsimd.memset(ones[:], 1.0)
-
         flipped_of = {}
         grouped_of = {}
         codes_of = {}
@@ -263,22 +255,12 @@ def tile_progenattention_pa_t_kernel(
                     in_=banks_of[V, chunk, pair][:].rearrange("p c (h d) -> p c h d", h=HEADS),
                 )
 
-        def is_vectors(which, chunk):
-            return which == K and chunk % VECTOR_SHARE == VECTOR_SHARE - 1
-
         def copy_others(which, chunk):
             place = chunk % CHUNKS * CHUNK
-            out = out_of[which, chunk // CHUNKS][:, place : place + CHUNK, :, ROT:HEAD_DIM]
-            in_ = banks_of[which, chunk, 1][:].rearrange("p c (h i) -> p c h i", h=HEADS)
-            if is_vectors(which, chunk):
-                nc.vector.tensor_tensor(
-                    out=out,
-                    in0=in_,
-                    in1=ones[:].unsqueeze(2).unsqueeze(3).to_broadcast([P, CHUNK, HEADS, ROT]),
-                    op=ALU.mult,
-                )
-            else:
-                nc.scalar.copy(out=out, in_=in_)
+            nc.scalar.copy(
+                out=out_of[which, chunk // CHUNKS][:, place : place + CHUNK, :, ROT:HEAD_DIM],
+                in_=banks_of[which, chunk, 1][:].rearrange("p c (h i) -> p c h i", h=HEADS),
+            )
 
         def rotate(which, chunk):
             direct = products.tile([P, CHUNK, HALF], F32)
@@ -311,7 +293,7 @@ def tile_progenattention_pa_t_kernel(
         def store(which, chunk):
             batch, place = divmod(chunk, CHUNKS)
             end = 0
-            for count in STORE_CHUNKS[which][batch]:
+            for count in STORE_CHUNKS[which]:
                 end += count
                 if place + 1 == end:
                     tiles = slice((end - count) * CHUNK, end * CHUNK)
@@ -343,15 +325,11 @@ def tile_progenattention_pa_t_kernel(
                 sines_and_cosines()
             for which in rotating:
                 rotate(which, chunk_of[which])
-                if not is_vectors(which, chunk_of[which]):
-                    copy_others(which, chunk_of[which])
+                copy_others(which, chunk_of[which])
             if V in chunk_of:
                 copy_values(chunk_of[V])
             if step + 3 < N_CHUNKS:
                 quantize_chunk(step + 3)
-            for which in rotating:
-                if is_vectors(which, chunk_of[which]):
-                    copy_others(which, chunk_of[which])
             if step == -AHEAD[V]:
                 pair_up_sines()
             for which in chunk_of:

@@ -30,7 +30,11 @@ Q, K, V = range(3)
 AHEAD = {Q: 1, K: 0, V: 2}
 WHOLE = [CHUNKS]
 HALVES = [CHUNKS // 2, CHUNKS // 2]
-STORE_CHUNKS = {Q: WHOLE, K: WHOLE, V: HALVES}
+STORE_CHUNKS = {
+    Q: [HALVES] * (BATCH - 1) + [WHOLE],
+    K: [HALVES] * (BATCH - 1) + [WHOLE],
+    V: [HALVES] * BATCH,
+}
 TWO_PI = 6.283185307179586
 ROUND = 12582912.0
 
@@ -293,7 +297,7 @@ def tile_progenattention_pa_t_kernel(
         def store(which, chunk):
             batch, place = divmod(chunk, CHUNKS)
             end = 0
-            for count in STORE_CHUNKS[which]:
+            for count in STORE_CHUNKS[which][batch]:
                 end += count
                 if place + 1 == end:
                     tiles = slice((end - count) * CHUNK, end * CHUNK)

from contextlib import ExitStack

import concourse.mybir as mybir
from concourse.masks import make_identity

F32 = mybir.dt.float32
BF16 = mybir.dt.bfloat16
I32 = mybir.dt.int32
U32 = mybir.dt.uint32
U8 = mybir.dt.uint8
FP8X4 = mybir.dt.float8_e4m3fn_x4
FP4X4 = mybir.dt.float4_e2m1fn_x4
ALU = mybir.AluOpType
ACT = mybir.ActivationFunctionType

P = 128
BATCH, SEQ, EMBED = 4, 2048, 512
HEADS, HEAD_DIM, ROT = 4, 64, 32
WIDTH = HEADS * HEAD_DIM
ANGLES = ROT // 2
SLOTS = SEQ // P
PAIR = 2
CHUNK = 4
CHUNKS = SLOTS // CHUNK
N_CHUNKS = BATCH * CHUNKS
PAIRS = CHUNK // PAIR
HALF = HEADS * ROT
LOADS = [CHUNK, CHUNK, 2 * CHUNK, SLOTS, 2 * SLOTS]
Q, K, V = range(3)
AHEAD = {Q: 1, K: 0, V: 2}
WHOLE = [CHUNKS]
HALVES = [CHUNKS // 2, CHUNKS // 2]
STORE_CHUNKS = {
    Q: [HALVES] * (BATCH - 1) + [WHOLE],
    K: [HALVES] * (BATCH - 1) + [WHOLE],
    V: [HALVES] * BATCH,
}
TWO_PI = 6.283185307179586
ROUND = 12582912.0

FLOPS = 2 * BATCH * SEQ * EMBED * 3 * WIDTH


def split_constant(value):
    scale = 1.0
    while value * scale < 2048.0:
        scale *= 2.0
    high = round(value * scale) / scale
    return high, value - high


def regroup_columns(nc, dst, src):
    blocks = dst.rearrange("p (n c) -> p n c", n=6)
    nc.gpsimd.tensor_copy(
        out=blocks[:, 4:6, :],
        in_=src.rearrange("p (g k c) -> p g k c", g=2, k=3)[:, :, 2, :],
    )
    natural = src.rearrange("p (g k s f w) -> p g k s f w", g=2, k=3, s=2, f=2)
    for kind in range(2):
        for half in range(2):
            nc.gpsimd.tensor_copy(
                out=blocks[:, 2 * kind + half, :].rearrange("p (g s w) -> p g s w", g=2, s=2),
                in_=natural[:, :, kind, :, half, :],
            )


def tile_progenattention_pa_t_kernel(
    tc, hidden_states, W_qkv_words, W_qkv_scales, out_0, out_1, out_2
):
    nc = tc.nc
    x_dram = hidden_states.rearrange("b (p t) e -> b p t e", t=SLOTS)
    out_dram = [o.rearrange("b (p t) h d -> b p t (h d)", t=SLOTS) for o in (out_0, out_1, out_2)]

    with ExitStack() as ctx:
        const = ctx.enter_context(tc.tile_pool(name="const", bufs=1))
        x_pool = ctx.enter_context(tc.tile_pool(name="x", bufs=1))
        grouped_pool = ctx.enter_context(tc.tile_pool(name="grouped", bufs=3))
        codes_pool = ctx.enter_context(tc.tile_pool(name="codes", bufs=5))
        products = ctx.enter_context(tc.tile_pool(name="products", bufs=4))
        out_pool = ctx.enter_context(tc.tile_pool(name="out", bufs=2))
        flipped_pool = ctx.enter_context(tc.psum_pool(name="flipped", bufs=2))
        banks = ctx.enter_context(tc.psum_pool(name="banks", bufs=6))
        ctx.enter_context(tc.manual_schedule())

        x_of = {}

        def load(n):
            first, count = sum(LOADS[:n]), LOADS[n]
            batch, slot = divmod(first, SLOTS)
            whole = max(count // SLOTS, 1)
            x_sb = x_pool.tile([P, count, EMBED], BF16, name="x_%d" % n)
            nc.sync.dma_start(
                out=x_sb[:].rearrange("p (b t) e -> p b t e", b=whole),
                in_=x_dram[batch : batch + whole, :, slot : slot + count // whole, :].rearrange(
                    "b p t e -> p b t e"
                ),
            )
            for place in range(count):
                x_of[first + place] = (x_sb, place)

        w_scales_in = const.tile([P, 3 * WIDTH], U8, align_bytes=64)
        nc.vector.memset(w_scales_in[:].bitcast(I32), 0)
        w_words_in = const.tile([P, 2 * 3 * WIDTH], U8, align_bytes=64)
        load(0)
        for quadrant in range(4):
            nc.sync.dma_start(
                out=w_scales_in[32 * quadrant : 32 * quadrant + 4, :].bitcast(I32),
                in_=W_qkv_scales[0, 4 * quadrant : 4 * quadrant + 4, :].bitcast(I32),
            )
        nc.sync.dma_start(out=w_words_in[:].bitcast(I32), in_=W_qkv_words[0].bitcast(I32))
        for n in range(1, len(LOADS)):
            load(n)

        warm = const.tile([P, 1], F32)
        nc.vector.memset(warm[:], 0.0)
        nc.scalar.activation(out=warm[:], in_=warm[:], func=ACT.Sin)

        position = const.tile([P, SLOTS], F32)
        nc.gpsimd.iota(
            position[:], pattern=[[1, SLOTS]], base=0, channel_multiplier=SLOTS,
            allow_small_or_imprecise_dtypes=True,
        )
        ident = const.tile([P, P], F32)
        make_identity(nc, ident[:])

        turns_high = const.tile([P, SLOTS, ANGLES], F32)
        turns_low = const.tile([P, SLOTS, ANGLES], F32)
        for j in range(ANGLES):
            high, low = split_constant(1.0 / (10000.0 ** (2 * j / ROT)) / TWO_PI)
            nc.vector.tensor_scalar_mul(out=turns_high[:, :, j], in0=position[:], scalar1=high)
            nc.vector.tensor_scalar_mul(out=turns_low[:, :, j], in0=position[:], scalar1=low)

        def drop_whole_turns(name, turns):
            whole = const.tile([P, SLOTS, ANGLES], F32, name=name + "_whole")
            nc.vector.tensor_scalar(
                out=whole[:], in0=turns[:], scalar1=ROUND, scalar2=ROUND,
                op0=ALU.add, op1=ALU.subtract,
            )
            rest = const.tile([P, SLOTS, ANGLES], F32, name=name)
            nc.vector.tensor_tensor(out=rest[:], in0=turns[:], in1=whole[:], op=ALU.subtract)
            return rest

        high_rest = drop_whole_turns("high_rest", turns_high)
        turns = const.tile([P, SLOTS, ANGLES], F32)
        nc.vector.tensor_tensor(out=turns[:], in0=high_rest[:], in1=turns_low[:], op=ALU.add)
        sin_turns = drop_whole_turns("sin_turns", turns)
        abs_turns = const.tile([P, SLOTS, ANGLES], F32)
        nc.vector.scalar_tensor_tensor(
            out=abs_turns[:], in0=sin_turns[:], scalar=-1.0, in1=sin_turns[:],
            op0=ALU.mult, op1=ALU.max,
        )

        sin_table = const.tile([P, SLOTS, ANGLES, 2], F32)
        cos_table = const.tile([P, SLOTS, ROT], F32)

        sin_plain = const.tile([P, SLOTS, ANGLES], F32)

        def sines_and_cosines():
            nc.scalar.activation(out=sin_plain[:], in_=sin_turns[:], func=ACT.Sin, scale=TWO_PI)
            nc.scalar.activation(
                out=cos_table[:].rearrange("p t (j e) -> p t j e", e=2),
                in_=abs_turns[:].unsqueeze(3).to_broadcast([P, SLOTS, ANGLES, 2]),
                func=ACT.Sin,
                scale=-TWO_PI,
                bias=TWO_PI / 4.0,
            )

        def pair_up_sines():
            nc.vector.tensor_scalar_mul(out=sin_table[:, :, :, 0], in0=sin_plain[:], scalar1=-1.0)
            nc.vector.tensor_copy(out=sin_table[:, :, :, 1], in_=sin_plain[:])

        w_words = const.tile([P, 2 * 3 * WIDTH], U8, align_bytes=64)
        w_scales = const.tile([P, 3 * WIDTH], U8, align_bytes=64)
        regroup_columns(nc, w_scales[:].bitcast(I32), w_scales_in[:].bitcast(I32))
        regroup_columns(nc, w_words[:].bitcast(I32), w_words_in[:].bitcast(I32))

        flipped_of = {}
        grouped_of = {}
        codes_of = {}
        banks_of = {}
        out_of = {}

        def transpose_chunk(chunk):
            flipped_of[chunk] = []
            for pair in range(CHUNK // PAIR):
                flipped = flipped_pool.tile([P, PAIR, 2, P], F32, name="flipped", tag="flipped")
                for c in range(PAIR):
                    x_sb, place = x_of[chunk * CHUNK + pair * PAIR + c]
                    words = x_sb[:, place, :].bitcast(F32)
                    for odd in range(2):
                        nc.tensor.transpose(
                            flipped[:, c, odd, :], words[:, odd : EMBED // 2 : 2], ident[:]
                        )
                flipped_of[chunk].append(flipped)

        def group_chunk(chunk):
            grouped = grouped_pool.tile([P, CHUNK * P * 4], BF16, align_bytes=64)
            words = grouped[:].bitcast(F32).rearrange("p (n c r w) -> p n c r w", n=2, c=PAIR, w=2)
            for pair in range(CHUNK // PAIR):
                nc.scalar.copy(
                    out=words[:, pair], in_=flipped_of[chunk][pair][:].rearrange("p c w r -> p c r w")
                )
            grouped_of[chunk] = grouped

        def quantize_chunk(chunk):
            codes = codes_pool.tile([P, CHUNK * P], U32, align_bytes=64)
            scales = codes_pool.tile([P, CHUNK * P], U8, align_bytes=64)
            nc.vector.quantize_mx(
                out=codes[:].bitcast(FP8X4), scales=scales[:], in_=grouped_of[chunk][:]
            )
            codes_of[chunk] = (codes, scales)

        def multiply(out, tile, columns):
            codes, code_scales = codes_of[tile // CHUNK]
            tokens = slice(tile % CHUNK * P, (tile % CHUNK + 1) * P)
            nc.tensor.matmul_mx(
                out=out,
                lhsT=codes[:, tokens].bitcast(FP8X4),
                lhsT_scale=code_scales[:, tokens],
                rhs=w_words[:, 2 * columns.start : 2 * columns.stop].bitcast(FP4X4),
                rhs_scale=w_scales[:, columns],
                start=True,
                stop=True,
            )

        def open_output(which, chunk):
            if chunk % CHUNKS == 0:
                out_sb = out_pool.tile(
                    [P, SLOTS, HEADS, HEAD_DIM], F32, name="out_%d" % which, tag="out_%d" % which
                )
                out_of[which, chunk // CHUNKS] = out_sb

        def project(which, chunk):
            open_output(which, chunk)
            for half in range(2):
                bank = banks.tile([P, CHUNK, HALF], F32, name="bank", tag="bank")
                first = (2 * which + half) * HALF
                for c in range(CHUNK):
                    multiply(bank[:, c, :], chunk * CHUNK + c, slice(first, first + HALF))
                banks_of[which, chunk, half] = bank

        def project_values(chunk):
            open_output(V, chunk)
            for pair in range(PAIRS):
                bank = banks.tile([P, PAIR, WIDTH], F32, name="bank", tag="bank")
                for c in range(PAIR):
                    multiply(
                        bank[:, c, :],
                        chunk * CHUNK + pair * PAIR + c,
                        slice(2 * WIDTH, 3 * WIDTH),
                    )
                banks_of[V, chunk, pair] = bank

        def copy_values(chunk):
            for pair in range(PAIRS):
                place = chunk % CHUNKS * CHUNK + pair * PAIR
                nc.scalar.copy(
                    out=out_of[V, chunk // CHUNKS][:, place : place + PAIR, :, :],
                    in_=banks_of[V, chunk, pair][:].rearrange("p c (h d) -> p c h d", h=HEADS),
                )

        def copy_others(which, chunk):
            place = chunk % CHUNKS * CHUNK
            nc.scalar.copy(
                out=out_of[which, chunk // CHUNKS][:, place : place + CHUNK, :, ROT:HEAD_DIM],
                in_=banks_of[which, chunk, 1][:].rearrange("p c (h i) -> p c h i", h=HEADS),
            )

        def rotate(which, chunk):
            direct = products.tile([P, CHUNK, HALF], F32)
            cross = products.tile([P, CHUNK, HALF], F32)
            rotated = banks_of[which, chunk, 0]
            place = chunk % CHUNKS * CHUNK
            nc.vector.tensor_tensor(
                out=direct[:].rearrange("p c (h i) -> p c h i", i=ROT),
                in0=rotated[:].rearrange("p c (h i) -> p c h i", i=ROT),
                in1=cos_table[:, place : place + CHUNK, :]
                .unsqueeze(2)
                .to_broadcast([P, CHUNK, HEADS, ROT]),
                op=ALU.mult,
            )
            nc.vector.tensor_tensor(
                out=cross[:].rearrange("p c (h j e) -> p c h j e", j=ANGLES, e=2),
                in0=rotated[:].rearrange("p c (h j e) -> p c h j e", j=ANGLES, e=2)[:, :, :, :, ::-1],
                in1=sin_table[:, place : place + CHUNK, :, :]
                .unsqueeze(2)
                .to_broadcast([P, CHUNK, HEADS, ANGLES, 2]),
                op=ALU.mult,
            )
            nc.gpsimd.tensor_tensor(
                out=out_of[which, chunk // CHUNKS][:, place : place + CHUNK, :, 0:ROT],
                in0=direct[:].rearrange("p c (h i) -> p c h i", h=HEADS),
                in1=cross[:].rearrange("p c (h i) -> p c h i", h=HEADS),
                op=ALU.add,
            )

        def store(which, chunk):
            batch, place = divmod(chunk, CHUNKS)
            end = 0
            for count in STORE_CHUNKS[which][batch]:
                end += count
                if place + 1 == end:
                    tiles = slice((end - count) * CHUNK, end * CHUNK)
                    nc.sync.dma_start(
                        out=out_dram[which][batch, :, tiles, :],
                        in_=out_of[which, batch][:, tiles].rearrange("p c h d -> p c (h d)"),
                    )

        transpose_chunk(0)
        group_chunk(0)
        quantize_chunk(0)
        transpose_chunk(1)
        for step in range(-AHEAD[V], N_CHUNKS):
            chunk_of = {}
            for which in (Q, K, V):
                if 0 <= step + AHEAD[which] < N_CHUNKS:
                    chunk_of[which] = step + AHEAD[which]
            rotating = [which for which in (Q, K) if which in chunk_of]

            for which in rotating:
                project(which, chunk_of[which])
            if V in chunk_of:
                project_values(chunk_of[V])
            if step + 4 < N_CHUNKS:
                transpose_chunk(step + 4)
            if step + 3 < N_CHUNKS:
                group_chunk(step + 3)
            if step == -AHEAD[V]:
                sines_and_cosines()
            for which in rotating:
                rotate(which, chunk_of[which])
                copy_others(which, chunk_of[which])
            if V in chunk_of:
                copy_values(chunk_of[V])
            if step + 3 < N_CHUNKS:
                quantize_chunk(step + 3)
            if step == -AHEAD[V]:
                pair_up_sines()
            for which in chunk_of:
                store(which, chunk_of[which])
